import numpy as np
import ml_dtypes


def mxq(x, axis, fmt="e4m3"):
    dtype, down = {"e4m3": (ml_dtypes.float8_e4m3fn, 7), "e5m2": (ml_dtypes.float8_e5m2, 14)}[fmt]
    v = np.moveaxis(np.asarray(x, np.float32).astype(ml_dtypes.bfloat16).astype(np.float64), axis, -1)
    blocks = v.reshape(v.shape[:-1] + (-1, 32))
    amax = np.abs(blocks).max(-1, keepdims=True)
    byte = np.maximum(np.where(amax > 0, np.frexp(amax)[1] - 1 + 127, 0) - down, 1)
    scale = np.exp2(byte - 127.0)
    codes = (blocks / scale).astype(np.float32).astype(dtype).astype(np.float64)
    return np.moveaxis((codes * scale).reshape(v.shape), -1, axis)


WIDE = False


def mx_kscale(k):
    if not WIDE:
        return np.ones(k)
    levels = np.array([10, -10, 5, -5, 0])
    a = np.random.permutation(np.resize(levels, k // 512 * 4)).reshape(k // 512, 4)
    idx = np.arange(k)
    return np.exp2(a[idx // 512, idx % 128 // 32])


BF16 = ml_dtypes.bfloat16


def bf(x):
    return np.asarray(x, np.float32).astype(BF16)


def f64(x):
    return np.asarray(x).astype(np.float64)


I, H, B = 1024, 1024, 512
K = I + H


def sigmoid(v):
    return 1.0 / (1.0 + np.exp(-v))


def inverted_bump(v):
    return np.where(v > 0, 1.0, 0.0)


def bump(v):
    return np.where(v <= 0, 1.0, 0.0)


def setup_inputs():
    s = mx_kscale(K)[:I]
    sw = np.concatenate((s, np.ones(H)))

    def mk_w():
        return bf(np.random.standard_normal((H, K)) / np.sqrt(K) / sw)

    return {
        "x": bf(np.random.standard_normal((B, I)) * s),
        "h_prev": bf(np.random.standard_normal((B, H))),
        "potential_prev": bf(np.random.standard_normal((B, H)) * 0.5),
        "W_r": mk_w(), "b_r": bf(np.random.standard_normal(H) * 1.0),
        "W_z": mk_w(), "b_z": bf(np.random.standard_normal(H) * 0.5),
        "W_c": mk_w(), "b_c": bf(np.random.standard_normal(H) * 0.5),
        "tresh": bf(np.random.uniform(0.0, 1.0, H) * 0.3),
        "decay_rate": bf(np.random.uniform(0.0, 1.0, H) * 0.7 + 0.1),
    }


def reference(x, h_prev, potential_prev, W_r, b_r, W_z, b_z, W_c, b_c, tresh, decay_rate):
    x, h_prev = f64(x), f64(h_prev)
    combined = mxq(np.concatenate((x, h_prev), axis=1), 1, "e4m3")
    r = sigmoid((combined @ mxq(f64(W_r), 1, "e4m3").T) + f64(b_r))
    z = sigmoid((combined @ mxq(f64(W_z), 1, "e4m3").T) + f64(b_z))
    combined_r = np.concatenate((combined[:, :I], mxq(r * h_prev, 1, "e4m3")), axis=1)
    n = np.tanh((combined_r @ mxq(f64(W_c), 1, "e4m3").T) + f64(b_c))
    h_new = (1.0 - z) * h_prev + z * n
    potential = f64(potential_prev) + h_new
    gated = np.maximum(potential - f64(tresh), 0.0)
    activated = inverted_bump(gated) * potential
    potential_non_gated = (potential * bump(gated)) * f64(decay_rate)
    return activated, potential_non_gated

@@ -1,0 +1,309 @@
+from contextlib import ExitStack
+
+import concourse.mybir as mybir
+from concourse.masks import make_identity
+
+FLOPS = 3 * 2 * 512 * 1024 * 2048
+
+F32 = mybir.dt.float32
+BF16 = mybir.dt.bfloat16
+U32 = mybir.dt.uint32
+U8 = mybir.dt.uint8
+FP8X4 = mybir.dt.float8_e4m3fn_x4
+ACT = mybir.ActivationFunctionType
+ALU = mybir.AluOpType
+
+P = 128
+NB = 512
+MANUAL = False
+LOAD_BUFS = 8
+BT_ACT_LAG = 2
+BT_NG_LAG = 3
+
+
+def tile_pglu_b_kernel(
+    tc, x, h_prev, potential_prev, W_r, b_r, W_z, b_z, W_c, b_c, tresh, decay_rate, out_0, out_1
+):
+    nc = tc.nc
+    with ExitStack() as ctx:
+        if MANUAL:
+            ctx.enter_context(tc.manual_schedule())
+        consts = ctx.enter_context(tc.tile_pool(name="consts", bufs=1))
+        keep = ctx.enter_context(tc.tile_pool(name="keep", bufs=1))
+        loads = ctx.enter_context(tc.tile_pool(name="loads", bufs=LOAD_BUFS))
+        wq = ctx.enter_context(tc.tile_pool(name="wq", bufs=4))
+        work = ctx.enter_context(tc.tile_pool(name="work", bufs=4))
+        outs = ctx.enter_context(tc.tile_pool(name="outs", bufs=2))
+        tp_pool = ctx.enter_context(tc.psum_pool(name="tp", bufs=4))
+        bk_pool = ctx.enter_context(tc.psum_pool(name="bk", bufs=2))
+        acc_pool = ctx.enter_context(tc.psum_pool(name="acc", bufs=2))
+
+        vt = consts.tile([P, 256], BF16, name="vt")
+        nc.vector.memset(vt[:], 0.0)
+        vecs = [b_r, b_z, b_c, tresh, decay_rate]
+        for v in range(5):
+            nc.scalar.dma_start(out=vt[4 * v : 4 * v + 4, :], in_=vecs[v].rearrange("(a q) -> a q", a=4))
+        warm = consts.tile([P, 1], F32, name="warm")
+        nc.vector.memset(warm[:], 0.0)
+        nc.scalar.activation(out=warm[:], in_=warm[:], func=ACT.Sigmoid)
+        ident = consts.tile([P, P], F32, name="ident")
+        make_identity(nc, ident[:])
+
+        hg = keep.tile([P, 2, NB, 4], BF16, name="hg", align_bytes=64)
+        cw = keep.tile([P, 4, NB], U32, name="cw", align_bytes=64)
+        cs = keep.tile([P, 4, NB], U8, name="cs", align_bytes=64)
+        rw = keep.tile([P, 2, NB], U32, name="rw", align_bytes=64)
+        rs = keep.tile([P, 2, NB], U8, name="rs", align_bytes=64)
+        r_all = keep.tile([P, 8, NB], F32, name="r_all")
+        sT = keep.tile([P, 8, NB], F32, name="sT")
+
+        w_of = {"r": W_r, "z": W_z, "c": W_c}
+        units = [("r", a) for a in range(4)]
+        for a in range(4):
+            units.append(("c", a))
+            units.append(("z", a))
+        load_list = ["x", "h"] + units[:4] + ["pp"] + units[4:]
+        loaded = {}
+        state = {"next_load": 0}
+
+        def issue_load():
+            i = state["next_load"]
+            if i >= len(load_list):
+                return
+            key = load_list[i]
+            state["next_load"] = i + 1
+            t = loads.tile([P, 4096], BF16, name="ld", tag="ld")
+            if key == "x":
+                src = x.rearrange("(p b) k -> p b k", b=4)
+                dst = t[:].rearrange("p (b k) -> p b k", b=4)
+            elif key == "h":
+                src = h_prev.rearrange("(p b) k -> p b k", b=4)
+                dst = t[:].rearrange("p (b k) -> p b k", b=4)
+            elif key == "pp":
+                src = potential_prev.rearrange("(p b) k -> p b k", b=4)
+                dst = t[:].rearrange("p (b k) -> p b k", b=4)
+            else:
+                src = w_of[key[0]].rearrange("(a p e) k -> a p e k", a=4, e=2)[key[1]]
+                dst = t[:].rearrange("p (e k) -> p e k", e=2)
+            nc.sync.dma_start(out=dst, in_=src)
+            loaded[key] = t
+
+        for i in range(LOAD_BUFS):
+            issue_load()
+
+        def evac(eng, out, in_):
+            if eng == "s":
+                nc.scalar.copy(out=out, in_=in_)
+            else:
+                nc.vector.tensor_copy(out=out, in_=in_)
+
+        def four_transposes(words, first, alternate):
+            bank = tp_pool.tile([P, 4, P], F32, name="tpb", tag="tp")
+            for j in range(4):
+                if alternate and j < 2:
+                    cols = words[:, first : first + 2 * P].rearrange("p (q u) -> p u q", u=2)[:, j, :]
+                else:
+                    cols = words[:, first + P * j : first + P * (j + 1)]
+                nc.tensor.transpose(bank[:, j, :], cols, ident[:])
+            return bank
+
+        vw = consts.tile([P, 32], F32, name="vw")
+        vf = consts.tile([P, 64], F32, name="vf")
+        vh = consts.tile([P, 8], F32, name="vh")
+
+        def vectors_in():
+            vbank = tp_pool.tile([P, 4, P], F32, name="vbank", tag="tp")
+            nc.tensor.transpose(vbank[:, 0, :], vt[:].bitcast(F32), ident[:])
+            nc.vector.tensor_copy(out=vw[:], in_=vbank[:, 0, 0:32])
+            nc.vector.tensor_copy(out=vf[:], in_=vw[:].bitcast(BF16))
+            nc.vector.tensor_scalar_mul(out=vh[:], in0=vf[:, 8:16], scalar1=0.5)
+
+        def vcol(v, ti):
+            return vf[:, 8 * v + ti : 8 * v + ti + 1]
+
+        def activations_in(key, grouped, g0):
+            words = loaded[key][:].bitcast(F32)
+            gf = grouped[:].bitcast(F32)
+            for b in range(4):
+                bank = four_transposes(words, 512 * b, g0 == 0)
+                evac(
+                    "s" if b % 2 == 0 else "v",
+                    gf[:, :, P * b : P * (b + 1), :],
+                    bank[:].rearrange("q (g u) c -> q g c u", u=2),
+                )
+            issue_load()
+            for g in range(2):
+                nc.vector.quantize_mx(
+                    out=cw[:, g0 + g, :].bitcast(FP8X4),
+                    scales=cs[:, g0 + g, :],
+                    in_=grouped[:, g].rearrange("p c t -> p (c t)"),
+                )
+
+        xg = keep.tile([P, 2, NB, 4], BF16, name="xg", tag="xr", align_bytes=64)
+        activations_in("x", xg, 0)
+        activations_in("h", hg, 2)
+        vectors_in()
+
+        quantised = {}
+
+        def weights_in(unit):
+            words = loaded[unit][:].bitcast(F32)
+            pair = []
+            for e in range(2):
+                wg = wq.tile([P, 4, P, 4], BF16, name="wg", tag="wg", align_bytes=64)
+                gf = wg[:].bitcast(F32)
+                for half in range(2):
+                    bank = four_transposes(words, 1024 * e + 512 * half, half == 0)
+                    evac("s", gf[:, 2 * half : 2 * half + 2, :, :], bank[:].rearrange("q (g u) c -> q g c u", u=2))
+                pair.append(wg)
+            issue_load()
+            res = []
+            for e in range(2):
+                ww = wq.tile([P, 4, P], U32, name="ww", tag="ww", align_bytes=64)
+                ws = wq.tile([P, 4, P], U8, name="ws", tag="ws", align_bytes=64)
+                nc.vector.quantize_mx(
+                    out=ww[:].rearrange("p g c -> p (g c)").bitcast(FP8X4),
+                    scales=ws[:].rearrange("p g c -> p (g c)"),
+                    in_=pair[e][:].rearrange("p g c t -> p (g c t)"),
+                )
+                res.append((ww, ws))
+            quantised[unit] = res
+
+        def potential_in():
+            words = loaded["pp"][:].bitcast(F32)
+            for a in range(4):
+                bank = tp_pool.tile([P, 4, P], F32, name="ppb", tag="tp")
+                for b in range(4):
+                    nc.tensor.transpose(bank[:, b, :], words[:, 512 * b + P * a : 512 * b + P * (a + 1)], ident[:])
+                nc.vector.tensor_tensor(
+                    out=sT[:, 2 * a : 2 * a + 2, :],
+                    in0=bank[:].rearrange("q b c -> q (b c)").bitcast(BF16).rearrange("q (c e) -> q e c", e=2),
+                    in1=hg[:, a // 2, :, 2 * (a % 2) : 2 * (a % 2) + 2].rearrange("q c e -> q e c"),
+                    op=ALU.add,
+                )
+            issue_load()
+
+        held = {}
+
+        def passes(unit):
+            gate, a = unit
+            for e in range(2):
+                ti = 2 * a + e
+                ww, ws = quantised[unit][e]
+                acc = acc_pool.tile([P, NB], F32, name="acc", tag="acc")
+                for g in range(4):
+                    if gate == "c" and g >= 2:
+                        rhs, rsc = rw[:, g - 2, :], rs[:, g - 2, :]
+                    else:
+                        rhs, rsc = cw[:, g, :], cs[:, g, :]
+                    nc.tensor.matmul_mx(
+                        out=acc[:],
+                        lhsT=ww[:, g, :].bitcast(FP8X4),
+                        lhsT_scale=ws[:, g, :],
+                        rhs=rhs.bitcast(FP8X4),
+                        rhs_scale=rsc,
+                        start=(g == 0),
+                        stop=(g == 3),
+                    )
+                if gate == "r":
+                    nc.scalar.activation(out=r_all[:, ti, :], in_=acc[:], func=ACT.Sigmoid, bias=vcol(0, ti), scale=1.0)
+                elif gate == "c":
+                    d = work.tile([P, NB], F32, name="d", tag="d")
+                    nc.scalar.activation(out=d[:], in_=acc[:], func=ACT.Tanh, bias=vcol(2, ti), scale=1.0)
+                    held[("d", ti)] = d
+                else:
+                    zt = work.tile([P, NB], F32, name="zt", tag="zt")
+                    nc.scalar.activation(out=zt[:], in_=acc[:], func=ACT.Tanh, bias=vh[:, ti : ti + 1], scale=0.5)
+                    held[("z", ti)] = zt
+
+        def after_r(a):
+            if a % 2 == 0:
+                return
+            g = a // 2
+            if g == 0:
+                held["rhg"] = keep.tile([P, 2, NB, 4], BF16, name="rhg", tag="xr", align_bytes=64)
+            rhg = held["rhg"]
+            nc.vector.tensor_tensor(
+                out=rhg[:, g],
+                in0=r_all[:, 4 * g : 4 * g + 4, :].rearrange("p t c -> p c t"),
+                in1=hg[:, g],
+                op=ALU.mult,
+            )
+            nc.vector.quantize_mx(
+                out=rw[:, g, :].bitcast(FP8X4),
+                scales=rs[:, g, :],
+                in_=rhg[:, g].rearrange("p c t -> p (c t)"),
+            )
+
+        def after_c(a):
+            for e in range(2):
+                ti = 2 * a + e
+                d = held[("d", ti)]
+                nc.vector.tensor_tensor(out=d[:], in0=d[:], in1=hg[:, ti // 4, :, ti % 4], op=ALU.subtract)
+
+        def after_z(a):
+            for e in range(2):
+                ti = 2 * a + e
+                d = held[("d", ti)]
+                zt = held[("z", ti)]
+                nc.vector.scalar_tensor_tensor(out=d[:], in0=zt[:], scalar=1.0, in1=d[:], op0=ALU.add, op1=ALU.mult)
+                pot = work.tile([P, NB], F32, name="pot", tag="pot")
+                nc.vector.scalar_tensor_tensor(
+                    out=pot[:], in0=d[:], scalar=0.5, in1=sT[:, ti, :], op0=ALU.mult, op1=ALU.add
+                )
+                av = work.tile([P, NB], F32, name="av", tag="av")
+                nc.vector.scalar_tensor_tensor(
+                    out=av[:], in0=pot[:], scalar=vcol(3, ti), in1=pot[:], op0=ALU.is_gt, op1=ALU.mult
+                )
+                held[("pot", ti)] = pot
+                held[("av", ti)] = av
+            for e in range(2):
+                ti = 2 * a + e
+                pot = held[("pot", ti)]
+                ng = work.tile([P, NB], F32, name="ng", tag="ng")
+                nc.vector.tensor_scalar(
+                    out=ng[:], in0=pot[:], scalar1=vcol(3, ti), scalar2=vcol(4, ti), op0=ALU.is_le, op1=ALU.mult
+                )
+                nc.vector.tensor_tensor(out=ng[:], in0=ng[:], in1=pot[:], op=ALU.mult)
+                held[("ng", ti)] = ng
+
+        def back(kind, a, dram):
+            o = outs.tile([P, 4, 256], F32, name="o" + kind, tag="o" + kind)
+            for hb in range(2):
+                bank = bk_pool.tile([P, 2, 2, P], F32, name="bkb", tag="bk")
+                for b2 in range(2):
+                    for e in range(2):
+                        src = held[(kind, 2 * a + e)]
+                        b = 2 * hb + b2
+                        nc.tensor.transpose(bank[:, b2, e, :], src[:, P * b : P * (b + 1)], ident[:])
+                evac(
+                    "s",
+                    o[:, 2 * hb : 2 * hb + 2, :].rearrange("c b (q e) -> c b q e", e=2),
+                    bank[:].rearrange("c b e q -> c b q e"),
+                )
+            nc.sync.dma_start(out=dram.rearrange("(c b) h -> c b h", b=4)[:, :, 256 * a : 256 * (a + 1)], in_=o[:])
+
+        n_units = len(units)
+        backs = {}
+        for a in range(4):
+            iz = 5 + 2 * a
+            backs[iz + BT_ACT_LAG] = backs.get(iz + BT_ACT_LAG, []) + [("av", a, out_0)]
+            backs[iz + BT_NG_LAG] = backs.get(iz + BT_NG_LAG, []) + [("ng", a, out_1)]
+
+        weights_in(units[0])
+        for i in range(n_units + max(BT_ACT_LAG, BT_NG_LAG) + 1):
+            if i + 1 < n_units:
+                if units[i + 1] == ("c", 0):
+                    potential_in()
+                weights_in(units[i + 1])
+            for job in backs.get(i, []):
+                back(job[0], job[1], job[2])
+            if i < n_units:
+                passes(units[i])
+                gate, a = units[i]
+                if gate == "r":
+                    after_r(a)
+                elif gate == "c":
+                    after_c(a)
+                else:
+                    after_z(a)

@@ -15,10 +15,17 @@ ALU = mybir.AluOpType
 
 P = 128
 NB = 512
-MANUAL = False
+MANUAL = True
 LOAD_BUFS = 8
-BT_ACT_LAG = 2
-BT_NG_LAG = 3
+SPLIT_LOADS = 4
+UNITS = [("r", 0), ("r", 1), ("r", 2), ("r", 3), ("z", 0), ("c", 0), ("c", 1), ("z", 1), ("c", 2), ("z", 2), ("c", 3), ("z", 3)]
+PP_AT = {2: (0, 1), 3: (2, 3)}
+LAG_P1 = 1
+LAG_P2 = 2
+LAG_BA = 2
+LAG_BN = 3
+PD_ON_SCALAR = (2, 3)
+HEAD_WOVEN = True
 
 
 def tile_pglu_b_kernel(
@@ -58,11 +65,9 @@ def tile_pglu_b_kernel(
         sT = keep.tile([P, 8, NB], F32, name="sT")
 
         w_of = {"r": W_r, "z": W_z, "c": W_c}
-        units = [("r", a) for a in range(4)]
-        for a in range(4):
-            units.append(("c", a))
-            units.append(("z", a))
-        load_list = ["x", "h"] + units[:4] + ["pp"] + units[4:]
+        a_of = {"x": x, "h": h_prev, "pp": potential_prev}
+        load_list = ["x", "h"] + UNITS[:4] + ["pp"] + UNITS[4:]
+        pp_sb = keep.tile([P, 4096], BF16, name="pp_sb")
         loaded = {}
         state = {"next_load": 0}
 
@@ -72,23 +77,25 @@ def tile_pglu_b_kernel(
                 return
             key = load_list[i]
             state["next_load"] = i + 1
-            t = loads.tile([P, 4096], BF16, name="ld", tag="ld")
-            if key == "x":
-                src = x.rearrange("(p b) k -> p b k", b=4)
-                dst = t[:].rearrange("p (b k) -> p b k", b=4)
-            elif key == "h":
-                src = h_prev.rearrange("(p b) k -> p b k", b=4)
-                dst = t[:].rearrange("p (b k) -> p b k", b=4)
-            elif key == "pp":
-                src = potential_prev.rearrange("(p b) k -> p b k", b=4)
+            if key == "pp":
+                t = pp_sb
+            else:
+                t = loads.tile([P, 4096], BF16, name="ld", tag="ld")
+            if key in a_of:
+                src = a_of[key].rearrange("(p b) k -> p b k", b=4)
                 dst = t[:].rearrange("p (b k) -> p b k", b=4)
             else:
                 src = w_of[key[0]].rearrange("(a p e) k -> a p e k", a=4, e=2)[key[1]]
                 dst = t[:].rearrange("p (e k) -> p e k", e=2)
-            nc.sync.dma_start(out=dst, in_=src)
+            n = dst.shape[1]
+            if i < SPLIT_LOADS:
+                nc.sync.dma_start(out=dst[:, : n // 2, :], in_=src[:, : n // 2, :])
+                nc.sync.dma_start(out=dst[:, n // 2 :, :], in_=src[:, n // 2 :, :])
+            else:
+                nc.sync.dma_start(out=dst, in_=src)
             loaded[key] = t
 
-        for i in range(LOAD_BUFS):
+        for i in range(LOAD_BUFS + 1):
             issue_load()
 
         def evac(eng, out, in_):
@@ -139,57 +146,53 @@ def tile_pglu_b_kernel(
                     in_=grouped[:, g].rearrange("p c t -> p (c t)"),
                 )
 
-        xg = keep.tile([P, 2, NB, 4], BF16, name="xg", tag="xr", align_bytes=64)
-        activations_in("x", xg, 0)
-        activations_in("h", hg, 2)
-        vectors_in()
-
+        grouped_w = {}
         quantised = {}
 
-        def weights_in(unit):
+        def transposes_w(unit, e, engines):
             words = loaded[unit][:].bitcast(F32)
-            pair = []
-            for e in range(2):
-                wg = wq.tile([P, 4, P, 4], BF16, name="wg", tag="wg", align_bytes=64)
-                gf = wg[:].bitcast(F32)
-                for half in range(2):
-                    bank = four_transposes(words, 1024 * e + 512 * half, half == 0)
-                    evac("s", gf[:, 2 * half : 2 * half + 2, :, :], bank[:].rearrange("q (g u) c -> q g c u", u=2))
-                pair.append(wg)
-            issue_load()
-            res = []
-            for e in range(2):
-                ww = wq.tile([P, 4, P], U32, name="ww", tag="ww", align_bytes=64)
-                ws = wq.tile([P, 4, P], U8, name="ws", tag="ws", align_bytes=64)
-                nc.vector.quantize_mx(
-                    out=ww[:].rearrange("p g c -> p (g c)").bitcast(FP8X4),
-                    scales=ws[:].rearrange("p g c -> p (g c)"),
-                    in_=pair[e][:].rearrange("p g c t -> p (g c t)"),
+            wg = wq.tile([P, 4, P, 4], BF16, name="wg", tag="wg", align_bytes=64)
+            gf = wg[:].bitcast(F32)
+            for half in range(2):
+                bank = four_transposes(words, 1024 * e + 512 * half, half == 0)
+                evac(
+                    engines[half],
+                    gf[:, 2 * half : 2 * half + 2, :, :],
+                    bank[:].rearrange("q (g u) c -> q g c u", u=2),
                 )
-                res.append((ww, ws))
-            quantised[unit] = res
+            grouped_w[(unit, e)] = wg
+            if e == 1:
+                issue_load()
 
-        def potential_in():
+        def quantise_w(unit, e):
+            ww = wq.tile([P, 4, P], U32, name="ww", tag="ww", align_bytes=64)
+            ws = wq.tile([P, 4, P], U8, name="ws", tag="ws", align_bytes=64)
+            nc.vector.quantize_mx(
+                out=ww[:].rearrange("p g c -> p (g c)").bitcast(FP8X4),
+                scales=ws[:].rearrange("p g c -> p (g c)"),
+                in_=grouped_w[(unit, e)][:].rearrange("p g c t -> p (g c t)"),
+            )
+            quantised[(unit, e)] = (ww, ws)
+
+        def potential_in(a):
             words = loaded["pp"][:].bitcast(F32)
-            for a in range(4):
-                bank = tp_pool.tile([P, 4, P], F32, name="ppb", tag="tp")
-                for b in range(4):
-                    nc.tensor.transpose(bank[:, b, :], words[:, 512 * b + P * a : 512 * b + P * (a + 1)], ident[:])
-                nc.vector.tensor_tensor(
-                    out=sT[:, 2 * a : 2 * a + 2, :],
-                    in0=bank[:].rearrange("q b c -> q (b c)").bitcast(BF16).rearrange("q (c e) -> q e c", e=2),
-                    in1=hg[:, a // 2, :, 2 * (a % 2) : 2 * (a % 2) + 2].rearrange("q c e -> q e c"),
-                    op=ALU.add,
-                )
-            issue_load()
+            bank = bk_pool.tile([P, 4, P], F32, name="ppb", tag="bk")
+            for b in range(4):
+                nc.tensor.transpose(bank[:, b, :], words[:, 512 * b + P * a : 512 * b + P * (a + 1)], ident[:])
+            nc.vector.tensor_tensor(
+                out=sT[:, 2 * a : 2 * a + 2, :],
+                in0=bank[:].rearrange("q b c -> q (b c)").bitcast(BF16).rearrange("q (c e) -> q e c", e=2),
+                in1=hg[:, a // 2, :, 2 * (a % 2) : 2 * (a % 2) + 2].rearrange("q c e -> q e c"),
+                op=ALU.add,
+            )
 
         held = {}
 
-        def passes(unit):
+        def passes(unit, e):
             gate, a = unit
-            for e in range(2):
+            if True:
                 ti = 2 * a + e
-                ww, ws = quantised[unit][e]
+                ww, ws = quantised[(unit, e)]
                 acc = acc_pool.tile([P, NB], F32, name="acc", tag="acc")
                 for g in range(4):
                     if gate == "c" and g >= 2:
@@ -241,33 +244,53 @@ def tile_pglu_b_kernel(
                 d = held[("d", ti)]
                 nc.vector.tensor_tensor(out=d[:], in0=d[:], in1=hg[:, ti // 4, :, ti % 4], op=ALU.subtract)
 
-        def after_z(a):
-            for e in range(2):
-                ti = 2 * a + e
+        def part1(a):
+            tis = (2 * a, 2 * a + 1)
+            for ti in tis:
                 d = held[("d", ti)]
-                zt = held[("z", ti)]
-                nc.vector.scalar_tensor_tensor(out=d[:], in0=zt[:], scalar=1.0, in1=d[:], op0=ALU.add, op1=ALU.mult)
+                nc.vector.scalar_tensor_tensor(
+                    out=d[:], in0=held[("z", ti)][:], scalar=1.0, in1=d[:], op0=ALU.add, op1=ALU.mult
+                )
+            for ti in tis:
                 pot = work.tile([P, NB], F32, name="pot", tag="pot")
                 nc.vector.scalar_tensor_tensor(
-                    out=pot[:], in0=d[:], scalar=0.5, in1=sT[:, ti, :], op0=ALU.mult, op1=ALU.add
+                    out=pot[:], in0=held[("d", ti)][:], scalar=0.5, in1=sT[:, ti, :], op0=ALU.mult, op1=ALU.add
                 )
+                held[("pot", ti)] = pot
+            if a in PD_ON_SCALAR:
+                for ti in tis:
+                    ng = work.tile([P, NB], F32, name="ng", tag="ng")
+                    nc.scalar.activation(out=ng[:], in_=held[("pot", ti)][:], func=ACT.Copy, scale=vcol(4, ti))
+                    held[("ng", ti)] = ng
+            for ti in tis:
+                pot = held[("pot", ti)]
                 av = work.tile([P, NB], F32, name="av", tag="av")
                 nc.vector.scalar_tensor_tensor(
                     out=av[:], in0=pot[:], scalar=vcol(3, ti), in1=pot[:], op0=ALU.is_gt, op1=ALU.mult
                 )
-                held[("pot", ti)] = pot
                 held[("av", ti)] = av
-            for e in range(2):
-                ti = 2 * a + e
-                pot = held[("pot", ti)]
+
+        def part2(a):
+            tis = (2 * a, 2 * a + 1)
+            if a in PD_ON_SCALAR:
+                for ti in tis:
+                    ng = held[("ng", ti)]
+                    nc.vector.scalar_tensor_tensor(
+                        out=ng[:], in0=held[("pot", ti)][:], scalar=vcol(3, ti), in1=ng[:], op0=ALU.is_le, op1=ALU.mult
+                    )
+                return
+            for ti in tis:
                 ng = work.tile([P, NB], F32, name="ng", tag="ng")
                 nc.vector.tensor_scalar(
-                    out=ng[:], in0=pot[:], scalar1=vcol(3, ti), scalar2=vcol(4, ti), op0=ALU.is_le, op1=ALU.mult
+                    out=ng[:], in0=held[("pot", ti)][:], scalar1=vcol(3, ti), scalar2=vcol(4, ti),
+                    op0=ALU.is_le, op1=ALU.mult,
                 )
-                nc.vector.tensor_tensor(out=ng[:], in0=ng[:], in1=pot[:], op=ALU.mult)
                 held[("ng", ti)] = ng
+            for ti in tis:
+                ng = held[("ng", ti)]
+                nc.vector.tensor_tensor(out=ng[:], in0=ng[:], in1=held[("pot", ti)][:], op=ALU.mult)
 
-        def back(kind, a, dram):
+        def back(kind, a, dram, engines):
             o = outs.tile([P, 4, 256], F32, name="o" + kind, tag="o" + kind)
             for hb in range(2):
                 bank = bk_pool.tile([P, 2, 2, P], F32, name="bkb", tag="bk")
@@ -277,33 +300,71 @@ def tile_pglu_b_kernel(
                         b = 2 * hb + b2
                         nc.tensor.transpose(bank[:, b2, e, :], src[:, P * b : P * (b + 1)], ident[:])
                 evac(
-                    "s",
+                    engines[hb],
                     o[:, 2 * hb : 2 * hb + 2, :].rearrange("c b (q e) -> c b q e", e=2),
                     bank[:].rearrange("c b e q -> c b q e"),
                 )
-            nc.sync.dma_start(out=dram.rearrange("(c b) h -> c b h", b=4)[:, :, 256 * a : 256 * (a + 1)], in_=o[:])
+                if a == 3:
+                    nc.sync.dma_start(
+                        out=dram.rearrange("(c b) h -> c b h", b=4)[:, 2 * hb : 2 * hb + 2, 256 * a : 256 * (a + 1)],
+                        in_=o[:, 2 * hb : 2 * hb + 2, :],
+                    )
+            if a < 3:
+                nc.sync.dma_start(out=dram.rearrange("(c b) h -> c b h", b=4)[:, :, 256 * a : 256 * (a + 1)], in_=o[:])
 
-        n_units = len(units)
-        backs = {}
+        n_units = len(UNITS)
+        jobs = {}
+
+        def plan(i, job):
+            jobs[i] = jobs.get(i, []) + [job]
+
         for a in range(4):
-            iz = 5 + 2 * a
-            backs[iz + BT_ACT_LAG] = backs.get(iz + BT_ACT_LAG, []) + [("av", a, out_0)]
-            backs[iz + BT_NG_LAG] = backs.get(iz + BT_NG_LAG, []) + [("ng", a, out_1)]
+            done = max(UNITS.index(("c", a)), UNITS.index(("z", a)))
+            late = 1 if a == 3 else 0
+            plan(done + LAG_P1, ("p1", a))
+            plan(done + LAG_P2 - late, ("p2", a))
+            plan(done + LAG_BA, ("ba", a))
+            plan(done + LAG_BN - late, ("bn", a))
 
-        weights_in(units[0])
-        for i in range(n_units + max(BT_ACT_LAG, BT_NG_LAG) + 1):
+        xg = keep.tile([P, 2, NB, 4], BF16, name="xg", tag="xr", align_bytes=64)
+        activations_in("x", xg, 0)
+        activations_in("h", hg, 2)
+        transposes_w(UNITS[0], 0, "sv")
+        quantise_w(UNITS[0], 0)
+        transposes_w(UNITS[0], 1, "sv")
+        vectors_in()
+        quantise_w(UNITS[0], 1)
+        for i in range(n_units + 4):
+            todo = jobs.get(i, [])
+            for a in PP_AT.get(i, ()):
+                potential_in(a)
+            if i == 0 and HEAD_WOVEN:
+                for e in range(2):
+                    transposes_w(UNITS[1], e, "sv")
+                    quantise_w(UNITS[1], e)
+                    passes(UNITS[0], e)
+                continue
             if i + 1 < n_units:
-                if units[i + 1] == ("c", 0):
-                    potential_in()
-                weights_in(units[i + 1])
-            for job in backs.get(i, []):
-                back(job[0], job[1], job[2])
+                transposes_w(UNITS[i + 1], 0, "ss")
+                transposes_w(UNITS[i + 1], 1, "ss")
+            for job in todo:
+                if job[0] == "ba":
+                    back("av", job[1], out_0, "ss")
+                if job[0] == "bn":
+                    back("ng", job[1], out_1, "sv" if job[1] == 3 else "ss")
+            for job in todo:
+                if job[0] == "p1":
+                    part1(job[1])
+                if job[0] == "p2":
+                    part2(job[1])
+            if i + 1 < n_units:
+                quantise_w(UNITS[i + 1], 0)
+                quantise_w(UNITS[i + 1], 1)
             if i < n_units:
-                passes(units[i])
-                gate, a = units[i]
+                passes(UNITS[i], 0)
+                passes(UNITS[i], 1)
+                gate, a = UNITS[i]
                 if gate == "r":
                     after_r(a)
                 elif gate == "c":
                     after_c(a)
-                else:
-                    after_z(a)

@@ -15,17 +15,116 @@ ALU = mybir.AluOpType
 
 P = 128
 NB = 512
-MANUAL = True
 LOAD_BUFS = 8
-SPLIT_LOADS = 4
 UNITS = [("r", 0), ("r", 1), ("r", 2), ("r", 3), ("z", 0), ("c", 0), ("c", 1), ("z", 1), ("c", 2), ("z", 2), ("c", 3), ("z", 3)]
-PP_AT = {2: (0, 1), 3: (2, 3)}
-LAG_P1 = 1
-LAG_P2 = 2
-LAG_BA = 2
-LAG_BN = 3
-PD_ON_SCALAR = (2, 3)
-HEAD_WOVEN = True
+OPT = {"wfirst": True, "u1_evac": "ss", "early": 0, "pp_at": {2: (0,), 3: (1,), 4: (2,), 5: (3,)}, "split_back": False, "halved": (("r", 0), ("r", 1)), "scalar_decay": (2, 3)}
+
+
+def build_steps():
+    s = []
+    n = len(UNITS)
+    early = OPT["early"]
+    if OPT.get("wfirst"):
+        u0, u1 = UNITS[0], UNITS[1]
+        s.append(("LOADS", [(u0, "all"), "x", "h", (u1, "all"), (UNITS[2], "all"), (UNITS[3], "all"), "pp"]))
+        for e in range(2):
+            for half in range(2):
+                s.append(("T", u0, e, half, "sv"[half]))
+            s.append(("Q", u0, e))
+        s.append(("FREE", u0))
+        s.append(("A", "x"))
+        s.append(("Ah", "h", 0))
+        for g in range(2):
+            for e in range(2):
+                s.append(("M", u0, e, (g,)))
+        s.append(("Ah", "h", 1))
+        s.append(("Aq", "h"))
+        for e in range(2):
+            for half in range(2):
+                s.append(("T", u1, e, half, OPT["u1_evac"][half]))
+        s.append(("FREE", u1))
+        s.append(("VEC",))
+        for e in range(2):
+            s.append(("Q", u1, e))
+        for g in range(2, 4):
+            for e in range(2):
+                s.append(("M", u0, e, (g,)))
+        return s + body(1)
+    s.append(("LOADS", ["x"] + [(UNITS[i], "lo") for i in range(early)] + ["h"] + [(UNITS[i], "hi") for i in range(early)]))
+    s.append(("LOADS", [(UNITS[i], "all") for i in range(early, 4)] + ["pp"]))
+    s.append(("A", "x"))
+    for i in range(early):
+        for e in range(2):
+            s.append(("T", UNITS[i], e, 0, "sv"[e]))
+        for e in range(2):
+            s.append(("Qh", UNITS[i], e, 0))
+    for i in range(early):
+        for e in range(2):
+            s.append(("M", UNITS[i], e, (0, 1)))
+    s.append(("A", "h"))
+    s.append(("VEC",))
+    for i in range(early):
+        for e in range(2):
+            s.append(("T", UNITS[i], e, 1, "sv"[e]))
+        s.append(("FREE", UNITS[i]))
+        for e in range(2):
+            s.append(("Qh", UNITS[i], e, 1))
+    first = early
+    if early == 0:
+        for e in range(2):
+            for half in range(2):
+                s.append(("T", UNITS[0], e, half, "sv"[half]))
+            s.append(("Q", UNITS[0], e))
+        s.append(("FREE", UNITS[0]))
+    return s + body(0, first, early)
+
+
+def body(start, first=0, early=0):
+    s = []
+    n = len(UNITS)
+    plan = {}
+
+    def at(i, step):
+        plan[i] = plan.get(i, []) + [step]
+
+    for a in range(4):
+        done = max(UNITS.index(("c", a)), UNITS.index(("z", a)))
+        if a < 3:
+            at(done + 1, ("P1", a))
+            at(done + 2, ("P2", a))
+            at(done + 2, ("B", "av", a))
+            at(done + 3, ("B", "ng", a))
+    for i in range(start, n):
+        nxt = i + 1
+        todo = plan.get(i, [])
+        have_next = nxt < n and nxt >= max(first, 1)
+        for a in OPT["pp_at"].get(i, ()):
+            s.append(("PP", a))
+        if have_next:
+            for e in range(2):
+                for half in range(2):
+                    s.append(("T", UNITS[nxt], e, half, "s"))
+            s.append(("FREE", UNITS[nxt]))
+        backs = [t for t in todo if t[0] == "B"]
+        if not OPT["split_back"]:
+            s.extend(backs)
+        s.extend([t for t in todo if t[0] != "B"])
+        if have_next:
+            for e in range(2):
+                s.append(("Q", UNITS[nxt], e))
+        gs = (2, 3) if i < early else (0, 1, 2, 3)
+        s.append(("M", UNITS[i], 0, gs))
+        if OPT["split_back"]:
+            s.extend(backs)
+        s.append(("M", UNITS[i], 1, gs))
+        gate, a = UNITS[i]
+        if gate == "r" and a % 2 == 1:
+            s.append(("RH", a // 2))
+        if gate == "c":
+            s.append(("D", a))
+    s.extend(plan.get(n, []))
+    s.append(("LAST",))
+    return s
 
 
 def tile_pglu_b_kernel(
@@ -33,8 +132,7 @@ def tile_pglu_b_kernel(
 ):
     nc = tc.nc
     with ExitStack() as ctx:
-        if MANUAL:
-            ctx.enter_context(tc.manual_schedule())
+        ctx.enter_context(tc.manual_schedule())
         consts = ctx.enter_context(tc.tile_pool(name="consts", bufs=1))
         keep = ctx.enter_context(tc.tile_pool(name="keep", bufs=1))
         loads = ctx.enter_context(tc.tile_pool(name="loads", bufs=LOAD_BUFS))
@@ -55,6 +153,9 @@ def tile_pglu_b_kernel(
         nc.scalar.activation(out=warm[:], in_=warm[:], func=ACT.Sigmoid)
         ident = consts.tile([P, P], F32, name="ident")
         make_identity(nc, ident[:])
+        vw = consts.tile([P, 32], F32, name="vw")
+        vf = consts.tile([P, 64], F32, name="vf")
+        vh = consts.tile([P, 8], F32, name="vh")
 
         hg = keep.tile([P, 2, NB, 4], BF16, name="hg", align_bytes=64)
         cw = keep.tile([P, 4, NB], U32, name="cw", align_bytes=64)
@@ -63,40 +164,50 @@ def tile_pglu_b_kernel(
         rs = keep.tile([P, 2, NB], U8, name="rs", align_bytes=64)
         r_all = keep.tile([P, 8, NB], F32, name="r_all")
         sT = keep.tile([P, 8, NB], F32, name="sT")
+        pp_sb = keep.tile([P, 4096], BF16, name="pp_sb")
 
         w_of = {"r": W_r, "z": W_z, "c": W_c}
         a_of = {"x": x, "h": h_prev, "pp": potential_prev}
-        load_list = ["x", "h"] + UNITS[:4] + ["pp"] + UNITS[4:]
-        pp_sb = keep.tile([P, 4096], BF16, name="pp_sb")
         loaded = {}
-        state = {"next_load": 0}
+        held = {}
+        later = [(u, "all") for u in UNITS[4:]]
+        state = {"later": 0}
 
-        def issue_load():
-            i = state["next_load"]
-            if i >= len(load_list):
-                return
-            key = load_list[i]
-            state["next_load"] = i + 1
-            if key == "pp":
-                t = pp_sb
-            else:
-                t = loads.tile([P, 4096], BF16, name="ld", tag="ld")
-            if key in a_of:
-                src = a_of[key].rearrange("(p b) k -> p b k", b=4)
+        def load(item):
+            if item in a_of:
+                if item == "pp":
+                    t = pp_sb
+                else:
+                    t = loads.tile([P, 4096], BF16, name="ld", tag="ld")
+                loaded[item] = t
+                src = a_of[item].rearrange("(p b) k -> p b k", b=4)
                 dst = t[:].rearrange("p (b k) -> p b k", b=4)
-            else:
-                src = w_of[key[0]].rearrange("(a p e) k -> a p e k", a=4, e=2)[key[1]]
-                dst = t[:].rearrange("p (e k) -> p e k", e=2)
-            n = dst.shape[1]
-            if i < SPLIT_LOADS:
-                nc.sync.dma_start(out=dst[:, : n // 2, :], in_=src[:, : n // 2, :])
-                nc.sync.dma_start(out=dst[:, n // 2 :, :], in_=src[:, n // 2 :, :])
+                if item == "pp":
+                    nc.sync.dma_start(out=dst, in_=src)
+                else:
+                    nc.sync.dma_start(out=dst[:, 0:2, :], in_=src[:, 0:2, :])
+                    nc.sync.dma_start(out=dst[:, 2:4, :], in_=src[:, 2:4, :])
+                return
+            unit, part = item
+            if unit not in loaded:
+                loaded[unit] = loads.tile([P, 4096], BF16, name="ld", tag="ld")
+            src = w_of[unit[0]].rearrange("(a p e) k -> a p e k", a=4, e=2)[unit[1]]
+            dst = loaded[unit][:].rearrange("p (e k) -> p e k", e=2)
+            if part == "lo":
+                nc.sync.dma_start(out=dst[:, :, 0:1024], in_=src[:, :, 0:1024])
+            elif part == "hi":
+                nc.sync.dma_start(out=dst[:, :, 1024:2048], in_=src[:, :, 1024:2048])
+            elif unit in OPT["halved"]:
+                nc.sync.dma_start(out=dst[:, 0:1, :], in_=src[:, 0:1, :])
+                nc.sync.dma_start(out=dst[:, 1:2, :], in_=src[:, 1:2, :])
             else:
                 nc.sync.dma_start(out=dst, in_=src)
-            loaded[key] = t
 
-        for i in range(LOAD_BUFS + 1):
-            issue_load()
+        def next_load():
+            i = state["later"]
+            if i < len(later):
+                state["later"] = i + 1
+                load(later[i])
 
         def evac(eng, out, in_):
             if eng == "s":
@@ -114,10 +225,6 @@ def tile_pglu_b_kernel(
                 nc.tensor.transpose(bank[:, j, :], cols, ident[:])
             return bank
 
-        vw = consts.tile([P, 32], F32, name="vw")
-        vf = consts.tile([P, 64], F32, name="vf")
-        vh = consts.tile([P, 8], F32, name="vh")
-
         def vectors_in():
             vbank = tp_pool.tile([P, 4, P], F32, name="vbank", tag="tp")
             nc.tensor.transpose(vbank[:, 0, :], vt[:].bitcast(F32), ident[:])
@@ -128,17 +235,28 @@ def tile_pglu_b_kernel(
         def vcol(v, ti):
             return vf[:, 8 * v + ti : 8 * v + ti + 1]
 
-        def activations_in(key, grouped, g0):
+        def activations_in(key, bs, quantise):
+            if key == "x":
+                if "xg" not in held:
+                    held["xg"] = keep.tile([P, 2, NB, 4], BF16, name="xg", tag="xr", align_bytes=64)
+                grouped = held["xg"]
+                g0 = 0
+            else:
+                grouped = hg
+                g0 = 2
             words = loaded[key][:].bitcast(F32)
             gf = grouped[:].bitcast(F32)
-            for b in range(4):
+            for b in bs:
                 bank = four_transposes(words, 512 * b, g0 == 0)
                 evac(
                     "s" if b % 2 == 0 else "v",
                     gf[:, :, P * b : P * (b + 1), :],
                     bank[:].rearrange("q (g u) c -> q g c u", u=2),
                 )
-            issue_load()
+            if 3 in bs:
+                next_load()
+            if not quantise:
+                return
             for g in range(2):
                 nc.vector.quantize_mx(
                     out=cw[:, g0 + g, :].bitcast(FP8X4),
@@ -146,36 +264,28 @@ def tile_pglu_b_kernel(
                     in_=grouped[:, g].rearrange("p c t -> p (c t)"),
                 )
 
-        grouped_w = {}
-        quantised = {}
-
-        def transposes_w(unit, e, engines):
+        def transposes_w(unit, e, half, eng):
             words = loaded[unit][:].bitcast(F32)
-            wg = wq.tile([P, 4, P, 4], BF16, name="wg", tag="wg", align_bytes=64)
-            gf = wg[:].bitcast(F32)
-            for half in range(2):
-                bank = four_transposes(words, 1024 * e + 512 * half, half == 0)
-                evac(
-                    engines[half],
-                    gf[:, 2 * half : 2 * half + 2, :, :],
-                    bank[:].rearrange("q (g u) c -> q g c u", u=2),
-                )
-            grouped_w[(unit, e)] = wg
-            if e == 1:
-                issue_load()
+            if (unit, e) not in held:
+                held[(unit, e)] = wq.tile([P, 4, P, 4], BF16, name="wg", tag="wg", align_bytes=64)
+            gf = held[(unit, e)][:].bitcast(F32)
+            bank = four_transposes(words, 1024 * e + 512 * half, half == 0)
+            evac(eng, gf[:, 2 * half : 2 * half + 2, :, :], bank[:].rearrange("q (g u) c -> q g c u", u=2))
 
-        def quantise_w(unit, e):
-            ww = wq.tile([P, 4, P], U32, name="ww", tag="ww", align_bytes=64)
-            ws = wq.tile([P, 4, P], U8, name="ws", tag="ws", align_bytes=64)
+        def quantise_w(unit, e, g_lo, g_hi):
+            if ("q", unit, e) not in held:
+                ww_new = wq.tile([P, 4, P], U32, name="ww", tag="ww", align_bytes=64)
+                ws_new = wq.tile([P, 4, P], U8, name="ws", tag="ws", align_bytes=64)
+                held[("q", unit, e)] = (ww_new, ws_new)
+            ww, ws = held[("q", unit, e)]
             nc.vector.quantize_mx(
-                out=ww[:].rearrange("p g c -> p (g c)").bitcast(FP8X4),
-                scales=ws[:].rearrange("p g c -> p (g c)"),
-                in_=grouped_w[(unit, e)][:].rearrange("p g c t -> p (g c t)"),
+                out=ww[:, g_lo:g_hi, :].rearrange("p g c -> p (g c)").bitcast(FP8X4),
+                scales=ws[:, g_lo:g_hi, :].rearrange("p g c -> p (g c)"),
+                in_=held[(unit, e)][:, g_lo:g_hi].rearrange("p g c t -> p (g c t)"),
             )
-            quantised[(unit, e)] = (ww, ws)
 
         def potential_in(a):
-            words = loaded["pp"][:].bitcast(F32)
+            words = pp_sb[:].bitcast(F32)
             bank = bk_pool.tile([P, 4, P], F32, name="ppb", tag="bk")
             for b in range(4):
                 nc.tensor.transpose(bank[:, b, :], words[:, 512 * b + P * a : 512 * b + P * (a + 1)], ident[:])
@@ -186,43 +296,41 @@ def tile_pglu_b_kernel(
                 op=ALU.add,
             )
 
-        held = {}
-
-        def passes(unit, e):
+        def passes(unit, e, gs):
             gate, a = unit
-            if True:
-                ti = 2 * a + e
-                ww, ws = quantised[(unit, e)]
-                acc = acc_pool.tile([P, NB], F32, name="acc", tag="acc")
-                for g in range(4):
-                    if gate == "c" and g >= 2:
-                        rhs, rsc = rw[:, g - 2, :], rs[:, g - 2, :]
-                    else:
-                        rhs, rsc = cw[:, g, :], cs[:, g, :]
-                    nc.tensor.matmul_mx(
-                        out=acc[:],
-                        lhsT=ww[:, g, :].bitcast(FP8X4),
-                        lhsT_scale=ws[:, g, :],
-                        rhs=rhs.bitcast(FP8X4),
-                        rhs_scale=rsc,
-                        start=(g == 0),
-                        stop=(g == 3),
-                    )
-                if gate == "r":
-                    nc.scalar.activation(out=r_all[:, ti, :], in_=acc[:], func=ACT.Sigmoid, bias=vcol(0, ti), scale=1.0)
-                elif gate == "c":
-                    d = work.tile([P, NB], F32, name="d", tag="d")
-                    nc.scalar.activation(out=d[:], in_=acc[:], func=ACT.Tanh, bias=vcol(2, ti), scale=1.0)
-                    held[("d", ti)] = d
+            ti = 2 * a + e
+            ww, ws = held[("q", unit, e)]
+            if gs[0] == 0:
+                held[("acc", unit, e)] = acc_pool.tile([P, NB], F32, name="acc", tag="acc")
+            acc = held[("acc", unit, e)]
+            for g in gs:
+                if gate == "c" and g >= 2:
+                    rhs, rsc = rw[:, g - 2, :], rs[:, g - 2, :]
                 else:
-                    zt = work.tile([P, NB], F32, name="zt", tag="zt")
-                    nc.scalar.activation(out=zt[:], in_=acc[:], func=ACT.Tanh, bias=vh[:, ti : ti + 1], scale=0.5)
-                    held[("z", ti)] = zt
-
-        def after_r(a):
-            if a % 2 == 0:
+                    rhs, rsc = cw[:, g, :], cs[:, g, :]
+                nc.tensor.matmul_mx(
+                    out=acc[:],
+                    lhsT=ww[:, g, :].bitcast(FP8X4),
+                    lhsT_scale=ws[:, g, :],
+                    rhs=rhs.bitcast(FP8X4),
+                    rhs_scale=rsc,
+                    start=(g == 0),
+                    stop=(g == 3),
+                )
+            if gs[-1] != 3:
                 return
-            g = a // 2
+            if gate == "r":
+                nc.scalar.activation(out=r_all[:, ti, :], in_=acc[:], func=ACT.Sigmoid, bias=vcol(0, ti), scale=1.0)
+            elif gate == "c":
+                d = work.tile([P, NB], F32, name="d", tag="d")
+                nc.scalar.activation(out=d[:], in_=acc[:], func=ACT.Tanh, bias=vcol(2, ti), scale=1.0)
+                held[("d", ti)] = d
+            else:
+                zt = work.tile([P, NB], F32, name="zt", tag="zt")
+                nc.scalar.activation(out=zt[:], in_=acc[:], func=ACT.Tanh, bias=vh[:, ti : ti + 1], scale=0.5)
+                held[("z", ti)] = zt
+
+        def reset_times_hidden(g):
             if g == 0:
                 held["rhg"] = keep.tile([P, 2, NB, 4], BF16, name="rhg", tag="xr", align_bytes=64)
             rhg = held["rhg"]
@@ -238,133 +346,126 @@ def tile_pglu_b_kernel(
                 in_=rhg[:, g].rearrange("p c t -> p (c t)"),
             )
 
-        def after_c(a):
-            for e in range(2):
-                ti = 2 * a + e
+        def candidate_minus_hidden(a):
+            for ti in (2 * a, 2 * a + 1):
                 d = held[("d", ti)]
                 nc.vector.tensor_tensor(out=d[:], in0=d[:], in1=hg[:, ti // 4, :, ti % 4], op=ALU.subtract)
 
-        def part1(a):
+        def new_tiles(a):
+            for ti in (2 * a, 2 * a + 1):
+                for kind in ("pot", "av", "ng"):
+                    held[(kind, ti)] = work.tile([P, NB], F32, name=kind, tag=kind)
+
+        def part1(a, cols, scalar_decay):
             tis = (2 * a, 2 * a + 1)
             for ti in tis:
                 d = held[("d", ti)]
                 nc.vector.scalar_tensor_tensor(
-                    out=d[:], in0=held[("z", ti)][:], scalar=1.0, in1=d[:], op0=ALU.add, op1=ALU.mult
+                    out=d[:, cols], in0=held[("z", ti)][:, cols], scalar=1.0, in1=d[:, cols], op0=ALU.add, op1=ALU.mult
                 )
             for ti in tis:
-                pot = work.tile([P, NB], F32, name="pot", tag="pot")
                 nc.vector.scalar_tensor_tensor(
-                    out=pot[:], in0=held[("d", ti)][:], scalar=0.5, in1=sT[:, ti, :], op0=ALU.mult, op1=ALU.add
+                    out=held[("pot", ti)][:, cols], in0=held[("d", ti)][:, cols], scalar=0.5, in1=sT[:, ti, cols],
+                    op0=ALU.mult, op1=ALU.add,
                 )
-                held[("pot", ti)] = pot
-            if a in PD_ON_SCALAR:
+            if scalar_decay:
                 for ti in tis:
-                    ng = work.tile([P, NB], F32, name="ng", tag="ng")
-                    nc.scalar.activation(out=ng[:], in_=held[("pot", ti)][:], func=ACT.Copy, scale=vcol(4, ti))
-                    held[("ng", ti)] = ng
+                    nc.scalar.activation(
+                        out=held[("ng", ti)][:, cols], in_=held[("pot", ti)][:, cols], func=ACT.Copy, scale=vcol(4, ti)
+                    )
             for ti in tis:
                 pot = held[("pot", ti)]
-                av = work.tile([P, NB], F32, name="av", tag="av")
                 nc.vector.scalar_tensor_tensor(
-                    out=av[:], in0=pot[:], scalar=vcol(3, ti), in1=pot[:], op0=ALU.is_gt, op1=ALU.mult
+                    out=held[("av", ti)][:, cols], in0=pot[:, cols], scalar=vcol(3, ti), in1=pot[:, cols],
+                    op0=ALU.is_gt, op1=ALU.mult,
                 )
-                held[("av", ti)] = av
 
-        def part2(a):
+        def part2(a, cols, scalar_decay):
             tis = (2 * a, 2 * a + 1)
-            if a in PD_ON_SCALAR:
+            if scalar_decay:
                 for ti in tis:
                     ng = held[("ng", ti)]
                     nc.vector.scalar_tensor_tensor(
-                        out=ng[:], in0=held[("pot", ti)][:], scalar=vcol(3, ti), in1=ng[:], op0=ALU.is_le, op1=ALU.mult
+                        out=ng[:, cols], in0=held[("pot", ti)][:, cols], scalar=vcol(3, ti), in1=ng[:, cols],
+                        op0=ALU.is_le, op1=ALU.mult,
                     )
                 return
             for ti in tis:
-                ng = work.tile([P, NB], F32, name="ng", tag="ng")
                 nc.vector.tensor_scalar(
-                    out=ng[:], in0=held[("pot", ti)][:], scalar1=vcol(3, ti), scalar2=vcol(4, ti),
-                    op0=ALU.is_le, op1=ALU.mult,
+                    out=held[("ng", ti)][:, cols], in0=held[("pot", ti)][:, cols], scalar1=vcol(3, ti),
+                    scalar2=vcol(4, ti), op0=ALU.is_le, op1=ALU.mult,
                 )
-                held[("ng", ti)] = ng
             for ti in tis:
                 ng = held[("ng", ti)]
-                nc.vector.tensor_tensor(out=ng[:], in0=ng[:], in1=held[("pot", ti)][:], op=ALU.mult)
+                nc.vector.tensor_tensor(out=ng[:, cols], in0=ng[:, cols], in1=held[("pot", ti)][:, cols], op=ALU.mult)
 
-        def back(kind, a, dram, engines):
-            o = outs.tile([P, 4, 256], F32, name="o" + kind, tag="o" + kind)
-            for hb in range(2):
-                bank = bk_pool.tile([P, 2, 2, P], F32, name="bkb", tag="bk")
-                for b2 in range(2):
-                    for e in range(2):
-                        src = held[(kind, 2 * a + e)]
-                        b = 2 * hb + b2
-                        nc.tensor.transpose(bank[:, b2, e, :], src[:, P * b : P * (b + 1)], ident[:])
-                evac(
-                    engines[hb],
-                    o[:, 2 * hb : 2 * hb + 2, :].rearrange("c b (q e) -> c b q e", e=2),
-                    bank[:].rearrange("c b e q -> c b q e"),
-                )
-                if a == 3:
-                    nc.sync.dma_start(
-                        out=dram.rearrange("(c b) h -> c b h", b=4)[:, 2 * hb : 2 * hb + 2, 256 * a : 256 * (a + 1)],
-                        in_=o[:, 2 * hb : 2 * hb + 2, :],
-                    )
-            if a < 3:
-                nc.sync.dma_start(out=dram.rearrange("(c b) h -> c b h", b=4)[:, :, 256 * a : 256 * (a + 1)], in_=o[:])
+        dram_of = {"av": out_0, "ng": out_1}
 
-        n_units = len(UNITS)
-        jobs = {}
-
-        def plan(i, job):
-            jobs[i] = jobs.get(i, []) + [job]
-
-        for a in range(4):
-            done = max(UNITS.index(("c", a)), UNITS.index(("z", a)))
-            late = 1 if a == 3 else 0
-            plan(done + LAG_P1, ("p1", a))
-            plan(done + LAG_P2 - late, ("p2", a))
-            plan(done + LAG_BA, ("ba", a))
-            plan(done + LAG_BN - late, ("bn", a))
-
-        xg = keep.tile([P, 2, NB, 4], BF16, name="xg", tag="xr", align_bytes=64)
-        activations_in("x", xg, 0)
-        activations_in("h", hg, 2)
-        transposes_w(UNITS[0], 0, "sv")
-        quantise_w(UNITS[0], 0)
-        transposes_w(UNITS[0], 1, "sv")
-        vectors_in()
-        quantise_w(UNITS[0], 1)
-        for i in range(n_units + 4):
-            todo = jobs.get(i, [])
-            for a in PP_AT.get(i, ()):
-                potential_in(a)
-            if i == 0 and HEAD_WOVEN:
+        def back_half(kind, a, hb, eng, store):
+            if hb == 0:
+                held[("o", kind)] = outs.tile([P, 4, 256], F32, name="o" + kind, tag="o" + kind)
+            o = held[("o", kind)]
+            bank = bk_pool.tile([P, 2, 2, P], F32, name="bkb", tag="bk")
+            for b2 in range(2):
                 for e in range(2):
-                    transposes_w(UNITS[1], e, "sv")
-                    quantise_w(UNITS[1], e)
-                    passes(UNITS[0], e)
-                continue
-            if i + 1 < n_units:
-                transposes_w(UNITS[i + 1], 0, "ss")
-                transposes_w(UNITS[i + 1], 1, "ss")
-            for job in todo:
-                if job[0] == "ba":
-                    back("av", job[1], out_0, "ss")
-                if job[0] == "bn":
-                    back("ng", job[1], out_1, "sv" if job[1] == 3 else "ss")
-            for job in todo:
-                if job[0] == "p1":
-                    part1(job[1])
-                if job[0] == "p2":
-                    part2(job[1])
-            if i + 1 < n_units:
-                quantise_w(UNITS[i + 1], 0)
-                quantise_w(UNITS[i + 1], 1)
-            if i < n_units:
-                passes(UNITS[i], 0)
-                passes(UNITS[i], 1)
-                gate, a = UNITS[i]
-                if gate == "r":
-                    after_r(a)
-                elif gate == "c":
-                    after_c(a)
+                    b = 2 * hb + b2
+                    nc.tensor.transpose(bank[:, b2, e, :], held[(kind, 2 * a + e)][:, P * b : P * (b + 1)], ident[:])
+            evac(
+                eng,
+                o[:, 2 * hb : 2 * hb + 2, :].rearrange("c b (q e) -> c b q e", e=2),
+                bank[:].rearrange("c b e q -> c b q e"),
+            )
+            view = dram_of[kind].rearrange("(c b) h -> c b h", b=4)
+            if store == "half":
+                nc.sync.dma_start(
+                    out=view[:, 2 * hb : 2 * hb + 2, 256 * a : 256 * (a + 1)], in_=o[:, 2 * hb : 2 * hb + 2, :]
+                )
+            elif hb == 1:
+                nc.sync.dma_start(out=view[:, :, 256 * a : 256 * (a + 1)], in_=o[:])
+
+        whole = slice(0, NB)
+        for step in build_steps():
+            kind = step[0]
+            if kind == "LOADS":
+                for item in step[1]:
+                    load(item)
+            elif kind == "A":
+                activations_in(step[1], (0, 1, 2, 3), True)
+            elif kind == "Ah":
+                activations_in(step[1], (2 * step[2], 2 * step[2] + 1), False)
+            elif kind == "Aq":
+                activations_in(step[1], (), True)
+            elif kind == "VEC":
+                vectors_in()
+            elif kind == "T":
+                transposes_w(step[1], step[2], step[3], step[4])
+            elif kind == "FREE":
+                next_load()
+            elif kind == "Q":
+                quantise_w(step[1], step[2], 0, 4)
+            elif kind == "Qh":
+                quantise_w(step[1], step[2], 2 * step[3], 2 * step[3] + 2)
+            elif kind == "M":
+                passes(step[1], step[2], step[3])
+            elif kind == "PP":
+                potential_in(step[1])
+            elif kind == "RH":
+                reset_times_hidden(step[1])
+            elif kind == "D":
+                candidate_minus_hidden(step[1])
+            elif kind == "P1":
+                new_tiles(step[1])
+                part1(step[1], whole, step[1] in OPT["scalar_decay"])
+            elif kind == "P2":
+                part2(step[1], whole, step[1] in OPT["scalar_decay"])
+            elif kind == "B":
+                for hb in range(2):
+                    back_half(step[1], step[2], hb, "s", "whole")
+            elif kind == "LAST":
+                new_tiles(3)
+                for hb in range(2):
+                    cols = slice(256 * hb, 256 * (hb + 1))
+                    part1(3, cols, True)
+                    part2(3, cols, True)
+                    back_half("av", 3, hb, "s", "half")
+                    back_half("ng", 3, hb, "s" if hb == 0 else "v", "half")

@@ -17,7 +17,7 @@ P = 128
 NB = 512
 LOAD_BUFS = 8
 UNITS = [("r", 0), ("r", 1), ("r", 2), ("r", 3), ("z", 0), ("c", 0), ("c", 1), ("z", 1), ("c", 2), ("z", 2), ("c", 3), ("z", 3)]
-OPT = {"wfirst": True, "u1_evac": "ss", "early": 0, "pp_at": {2: (0,), 3: (1,), 4: (2,), 5: (3,)}, "split_back": False, "halved": (("r", 0), ("r", 1)), "scalar_decay": (2, 3)}
+OPT = {"wfirst": True, "u1_evac": "ss", "early": 0, "pp_at": {2: (0,), 3: (1,), 4: (2,), 5: (3,)}, "split_back": False, "halved": (("r", 0), ("r", 1)), "scalar_decay": (2, 3), "warm": (5, 1, 1, 1, 1)}
 
 
 def build_steps():
@@ -27,13 +27,26 @@ def build_steps():
     if OPT.get("wfirst"):
         u0, u1 = UNITS[0], UNITS[1]
         s.append(("LOADS", [(u0, "all"), "x", "h", (u1, "all"), (UNITS[2], "all"), (UNITS[3], "all"), "pp"]))
+        w = OPT.get("warm", (0, 0, 0, 0, 0))
+        if w[0]:
+            s.append(("WARM", w[0]))
         for e in range(2):
             for half in range(2):
                 s.append(("T", u0, e, half, "sv"[half]))
             s.append(("Q", u0, e))
+            if w[1]:
+                s.append(("WARM", w[1]))
         s.append(("FREE", u0))
-        s.append(("A", "x"))
+        s.append(("Ah", "x", 0))
+        if w[2]:
+            s.append(("WARM", w[2]))
+        s.append(("Ah", "x", 1))
+        s.append(("Aq", "x"))
+        if w[3]:
+            s.append(("WARM", w[3]))
         s.append(("Ah", "h", 0))
+        if w[4]:
+            s.append(("WARM", w[4]))
         for g in range(2):
             for e in range(2):
                 s.append(("M", u0, e, (g,)))
@@ -423,10 +436,20 @@ def tile_pglu_b_kernel(
             elif hb == 1:
                 nc.sync.dma_start(out=view[:, :, 256 * a : 256 * (a + 1)], in_=o[:])
 
+        zeros = consts.tile([P, NB], BF16, name="zeros")
+        nc.vector.memset(zeros[:], 0.0)
+
+        def keep_clock(n):
+            idle = acc_pool.tile([P, NB], F32, name="idle", tag="acc")
+            for i in range(n):
+                nc.tensor.matmul(out=idle[:], lhsT=zeros[:, 0:P], rhs=zeros[:], start=True, stop=True)
+
         whole = slice(0, NB)
         for step in build_steps():
             kind = step[0]
-            if kind == "LOADS":
+            if kind == "WARM":
+                keep_clock(step[1])
+            elif kind == "LOADS":
                 for item in step[1]:
                     load(item)
             elif kind == "A":

@@ -17,7 +17,7 @@ P = 128
 NB = 512
 LOAD_BUFS = 8
 UNITS = [("r", 0), ("r", 1), ("r", 2), ("r", 3), ("z", 0), ("c", 0), ("c", 1), ("z", 1), ("c", 2), ("z", 2), ("c", 3), ("z", 3)]
-OPT = {"wfirst": True, "u1_evac": "ss", "early": 0, "pp_at": {2: (0,), 3: (1,), 4: (2,), 5: (3,)}, "split_back": False, "halved": (("r", 0), ("r", 1)), "scalar_decay": (2, 3), "warm": (5, 1, 1, 1, 1)}
+OPT = {"wfirst": True, "u1_evac": "ss", "early": 0, "pp_at": {2: (0,), 3: (1,), 4: (2,), 5: (3,)}, "split_back": False, "halved": (("r", 0), ("r", 1)), "scalar_decay": (2, 3)}
 
 
 def build_steps():
@@ -105,8 +105,9 @@ def body(start, first=0, early=0):
         if a < 3:
             at(done + 1, ("P1", a))
             at(done + 2, ("P2", a))
-            at(done + 2, ("B", "av", a))
-            at(done + 3, ("B", "ng", a))
+            if a not in OPT.get("defer", ()):
+                at(done + 2, ("B", "av", a))
+                at(done + 3, ("B", "ng", a))
     for i in range(start, n):
         nxt = i + 1
         todo = plan.get(i, [])
@@ -145,12 +146,12 @@ def tile_pglu_b_kernel(
 ):
     nc = tc.nc
     with ExitStack() as ctx:
-        ctx.enter_context(tc.manual_schedule())
         consts = ctx.enter_context(tc.tile_pool(name="consts", bufs=1))
         keep = ctx.enter_context(tc.tile_pool(name="keep", bufs=1))
         loads = ctx.enter_context(tc.tile_pool(name="loads", bufs=LOAD_BUFS))
         wq = ctx.enter_context(tc.tile_pool(name="wq", bufs=4))
         work = ctx.enter_context(tc.tile_pool(name="work", bufs=4))
+        late = ctx.enter_context(tc.tile_pool(name="late", bufs=OPT.get("late_bufs", 4)))
         outs = ctx.enter_context(tc.tile_pool(name="outs", bufs=2))
         tp_pool = ctx.enter_context(tc.psum_pool(name="tp", bufs=4))
         bk_pool = ctx.enter_context(tc.psum_pool(name="bk", bufs=2))
@@ -366,8 +367,9 @@ def tile_pglu_b_kernel(
 
         def new_tiles(a):
             for ti in (2 * a, 2 * a + 1):
-                for kind in ("pot", "av", "ng"):
-                    held[(kind, ti)] = work.tile([P, NB], F32, name=kind, tag=kind)
+                held[("pot", ti)] = work.tile([P, NB], F32, name="pot", tag="pot")
+                for kind in ("av", "ng"):
+                    held[(kind, ti)] = late.tile([P, NB], F32, name=kind, tag=kind)
 
         def part1(a, cols, scalar_decay):
             tis = (2 * a, 2 * a + 1)
@@ -490,5 +492,8 @@ def tile_pglu_b_kernel(
                     cols = slice(256 * hb, 256 * (hb + 1))
                     part1(3, cols, True)
                     part2(3, cols, True)
+                    for a in OPT.get("defer", ()):
+                        for hb2 in range(2):
+                            back_half(("av", "ng")[hb], a, hb2, "s", "whole")
                     back_half("av", 3, hb, "s", "half")
                     back_half("ng", 3, hb, "s" if hb == 0 else "v", "half")

@@ -14,131 +14,27 @@ ACT = mybir.ActivationFunctionType
 ALU = mybir.AluOpType
 
 P = 128
-NB = 512
-LOAD_BUFS = 8
-UNITS = [("r", 0), ("r", 1), ("r", 2), ("r", 3), ("z", 0), ("c", 0), ("c", 1), ("z", 1), ("c", 2), ("z", 2), ("c", 3), ("z", 3)]
-OPT = {"wfirst": True, "u1_evac": "ss", "early": 0, "pp_at": {2: (0,), 3: (1,), 4: (2,), 5: (3,)}, "split_back": False, "halved": (("r", 0), ("r", 1)), "scalar_decay": (2, 3)}
-
-
-def build_steps():
-    s = []
-    n = len(UNITS)
-    early = OPT["early"]
-    if OPT.get("wfirst"):
-        u0, u1 = UNITS[0], UNITS[1]
-        s.append(("LOADS", [(u0, "all"), "x", "h", (u1, "all"), (UNITS[2], "all"), (UNITS[3], "all"), "pp"]))
-        w = OPT.get("warm", (0, 0, 0, 0, 0))
-        if w[0]:
-            s.append(("WARM", w[0]))
-        for e in range(2):
-            for half in range(2):
-                s.append(("T", u0, e, half, "sv"[half]))
-            s.append(("Q", u0, e))
-            if w[1]:
-                s.append(("WARM", w[1]))
-        s.append(("FREE", u0))
-        s.append(("Ah", "x", 0))
-        if w[2]:
-            s.append(("WARM", w[2]))
-        s.append(("Ah", "x", 1))
-        s.append(("Aq", "x"))
-        if w[3]:
-            s.append(("WARM", w[3]))
-        s.append(("Ah", "h", 0))
-        if w[4]:
-            s.append(("WARM", w[4]))
-        for g in range(2):
-            for e in range(2):
-                s.append(("M", u0, e, (g,)))
-        s.append(("Ah", "h", 1))
-        s.append(("Aq", "h"))
-        for e in range(2):
-            for half in range(2):
-                s.append(("T", u1, e, half, OPT["u1_evac"][half]))
-        s.append(("FREE", u1))
-        s.append(("VEC",))
-        for e in range(2):
-            s.append(("Q", u1, e))
-        for g in range(2, 4):
-            for e in range(2):
-                s.append(("M", u0, e, (g,)))
-        return s + body(1)
-    s.append(("LOADS", ["x"] + [(UNITS[i], "lo") for i in range(early)] + ["h"] + [(UNITS[i], "hi") for i in range(early)]))
-    s.append(("LOADS", [(UNITS[i], "all") for i in range(early, 4)] + ["pp"]))
-    s.append(("A", "x"))
-    for i in range(early):
-        for e in range(2):
-            s.append(("T", UNITS[i], e, 0, "sv"[e]))
-        for e in range(2):
-            s.append(("Qh", UNITS[i], e, 0))
-    for i in range(early):
-        for e in range(2):
-            s.append(("M", UNITS[i], e, (0, 1)))
-    s.append(("A", "h"))
-    s.append(("VEC",))
-    for i in range(early):
-        for e in range(2):
-            s.append(("T", UNITS[i], e, 1, "sv"[e]))
-        s.append(("FREE", UNITS[i]))
-        for e in range(2):
-            s.append(("Qh", UNITS[i], e, 1))
-    first = early
-    if early == 0:
-        for e in range(2):
-            for half in range(2):
-                s.append(("T", UNITS[0], e, half, "sv"[half]))
-            s.append(("Q", UNITS[0], e))
-        s.append(("FREE", UNITS[0]))
-    return s + body(0, first, early)
-
-
-def body(start, first=0, early=0):
-    s = []
-    n = len(UNITS)
-    plan = {}
-
-    def at(i, step):
-        plan[i] = plan.get(i, []) + [step]
-
-    for a in range(4):
-        done = max(UNITS.index(("c", a)), UNITS.index(("z", a)))
-        if a < 3:
-            at(done + 1, ("P1", a))
-            at(done + 2, ("P2", a))
-            if a not in OPT.get("defer", ()):
-                at(done + 2, ("B", "av", a))
-                at(done + 3, ("B", "ng", a))
-    for i in range(start, n):
-        nxt = i + 1
-        todo = plan.get(i, [])
-        have_next = nxt < n and nxt >= max(first, 1)
-        for a in OPT["pp_at"].get(i, ()):
-            s.append(("PP", a))
-        if have_next:
-            for e in range(2):
-                for half in range(2):
-                    s.append(("T", UNITS[nxt], e, half, "s"))
-            s.append(("FREE", UNITS[nxt]))
-        backs = [t for t in todo if t[0] == "B"]
-        if not OPT["split_back"]:
-            s.extend(backs)
-        s.extend([t for t in todo if t[0] != "B"])
-        if have_next:
-            for e in range(2):
-                s.append(("Q", UNITS[nxt], e))
-        gs = (2, 3) if i < early else (0, 1, 2, 3)
-        s.append(("M", UNITS[i], 0, gs))
-        if OPT["split_back"]:
-            s.extend(backs)
-        s.append(("M", UNITS[i], 1, gs))
-        gate, a = UNITS[i]
-        if gate == "r" and a % 2 == 1:
-            s.append(("RH", a // 2))
-        if gate == "c":
-            s.append(("D", a))
-    s.extend(plan.get(n, []))
-    s.append(("LAST",))
-    return s
+BATCH = 512
+HALF = BATCH // 2
+CHUNK = 256
+PASSES = 4
+LOAD_COLS = 4096
+ROW_WORDS = 512
+PAIR_WORDS = 512
+MX_ALIGN = 64
+LOAD_SLOTS = 8
+ROUNDS = [
+    ("r", 0), ("r", 1), ("r", 2), ("r", 3),
+    ("z", 0), ("c", 0), ("c", 1), ("z", 1), ("c", 2), ("z", 2), ("c", 3), ("z", 3),
+]
+LAST_CHUNK = 3
+POTENTIAL_BEFORE = {2: 0, 3: 1, 4: 2, 5: 3}
+DECAY_ON_SCALAR = (2, 3)
+B_R = 0
+B_Z = 1
+B_C = 2
+TRESH = 3
+DECAY = 4
 
 
 def tile_pglu_b_kernel(
@@ -146,354 +42,363 @@ def tile_pglu_b_kernel(
 ):
     nc = tc.nc
     with ExitStack() as ctx:
+        ctx.enter_context(tc.manual_schedule())
         consts = ctx.enter_context(tc.tile_pool(name="consts", bufs=1))
         keep = ctx.enter_context(tc.tile_pool(name="keep", bufs=1))
-        loads = ctx.enter_context(tc.tile_pool(name="loads", bufs=LOAD_BUFS))
+        loads = ctx.enter_context(tc.tile_pool(name="loads", bufs=LOAD_SLOTS))
         wq = ctx.enter_context(tc.tile_pool(name="wq", bufs=4))
         work = ctx.enter_context(tc.tile_pool(name="work", bufs=4))
-        late = ctx.enter_context(tc.tile_pool(name="late", bufs=OPT.get("late_bufs", 4)))
         outs = ctx.enter_context(tc.tile_pool(name="outs", bufs=2))
         tp_pool = ctx.enter_context(tc.psum_pool(name="tp", bufs=4))
         bk_pool = ctx.enter_context(tc.psum_pool(name="bk", bufs=2))
         acc_pool = ctx.enter_context(tc.psum_pool(name="acc", bufs=2))
 
-        vt = consts.tile([P, 256], BF16, name="vt")
-        nc.vector.memset(vt[:], 0.0)
-        vecs = [b_r, b_z, b_c, tresh, decay_rate]
-        for v in range(5):
-            nc.scalar.dma_start(out=vt[4 * v : 4 * v + 4, :], in_=vecs[v].rearrange("(a q) -> a q", a=4))
+        vec_rows = consts.tile([P, CHUNK], BF16, name="vec_rows")
+        nc.vector.memset(vec_rows[:], 0.0)
         warm = consts.tile([P, 1], F32, name="warm")
         nc.vector.memset(warm[:], 0.0)
         nc.scalar.activation(out=warm[:], in_=warm[:], func=ACT.Sigmoid)
         ident = consts.tile([P, P], F32, name="ident")
         make_identity(nc, ident[:])
-        vw = consts.tile([P, 32], F32, name="vw")
-        vf = consts.tile([P, 64], F32, name="vf")
-        vh = consts.tile([P, 8], F32, name="vh")
+        for v, vec in enumerate((b_r, b_z, b_c, tresh, decay_rate)):
+            nc.gpsimd.dma_start(out=vec_rows[4 * v : 4 * v + 4, :], in_=vec.rearrange("(a q) -> a q", a=4))
+        vec_words = consts.tile([P, 32], F32, name="vec_words")
+        vec_f32 = consts.tile([P, 64], F32, name="vec_f32")
+        half_b_z = consts.tile([P, 8], F32, name="half_b_z")
 
-        hg = keep.tile([P, 2, NB, 4], BF16, name="hg", align_bytes=64)
-        cw = keep.tile([P, 4, NB], U32, name="cw", align_bytes=64)
-        cs = keep.tile([P, 4, NB], U8, name="cs", align_bytes=64)
-        rw = keep.tile([P, 2, NB], U32, name="rw", align_bytes=64)
-        rs = keep.tile([P, 2, NB], U8, name="rs", align_bytes=64)
-        r_all = keep.tile([P, 8, NB], F32, name="r_all")
-        sT = keep.tile([P, 8, NB], F32, name="sT")
-        pp_sb = keep.tile([P, 4096], BF16, name="pp_sb")
+        h_grouped = keep.tile([P, 2, BATCH, 4], BF16, name="h_grouped", align_bytes=MX_ALIGN)
+        act_codes = keep.tile([P, PASSES, BATCH], U32, name="act_codes", align_bytes=MX_ALIGN)
+        act_scales = keep.tile([P, PASSES, BATCH], U8, name="act_scales", align_bytes=MX_ALIGN)
+        rh_codes = keep.tile([P, 2, BATCH], U32, name="rh_codes", align_bytes=MX_ALIGN)
+        rh_scales = keep.tile([P, 2, BATCH], U8, name="rh_scales", align_bytes=MX_ALIGN)
+        r_all = keep.tile([P, 8, BATCH], F32, name="r_all")
+        base = keep.tile([P, 8, BATCH], F32, name="base")
+        pp_sb = keep.tile([P, LOAD_COLS], BF16, name="pp_sb")
 
-        w_of = {"r": W_r, "z": W_z, "c": W_c}
-        a_of = {"x": x, "h": h_prev, "pp": potential_prev}
+        weight_of = {"r": W_r, "z": W_z, "c": W_c}
         loaded = {}
         held = {}
-        later = [(u, "all") for u in UNITS[4:]]
-        state = {"later": 0}
+        progress = {"loads": 0}
 
-        def load(item):
-            if item in a_of:
-                if item == "pp":
-                    t = pp_sb
-                else:
-                    t = loads.tile([P, 4096], BF16, name="ld", tag="ld")
-                loaded[item] = t
-                src = a_of[item].rearrange("(p b) k -> p b k", b=4)
-                dst = t[:].rearrange("p (b k) -> p b k", b=4)
-                if item == "pp":
-                    nc.sync.dma_start(out=dst, in_=src)
-                else:
-                    nc.sync.dma_start(out=dst[:, 0:2, :], in_=src[:, 0:2, :])
-                    nc.sync.dma_start(out=dst[:, 2:4, :], in_=src[:, 2:4, :])
-                return
-            unit, part = item
-            if unit not in loaded:
-                loaded[unit] = loads.tile([P, 4096], BF16, name="ld", tag="ld")
-            src = w_of[unit[0]].rearrange("(a p e) k -> a p e k", a=4, e=2)[unit[1]]
+        def load_rows(key, source, tile_ap, in_halves):
+            loaded[key] = tile_ap
+            src = source.rearrange("(p b) k -> p b k", b=4)
+            dst = tile_ap[:].rearrange("p (b k) -> p b k", b=4)
+            if in_halves:
+                nc.sync.dma_start(out=dst[:, 0:2, :], in_=src[:, 0:2, :])
+                nc.sync.dma_start(out=dst[:, 2:4, :], in_=src[:, 2:4, :])
+            else:
+                nc.sync.dma_start(out=dst, in_=src)
+
+        def load_chunk(unit, in_halves):
+            loaded[unit] = loads.tile([P, LOAD_COLS], BF16, name="ld", tag="ld")
+            src = weight_of[unit[0]].rearrange("(a p e) k -> a p e k", a=4, e=2)[unit[1]]
             dst = loaded[unit][:].rearrange("p (e k) -> p e k", e=2)
-            if part == "lo":
-                nc.sync.dma_start(out=dst[:, :, 0:1024], in_=src[:, :, 0:1024])
-            elif part == "hi":
-                nc.sync.dma_start(out=dst[:, :, 1024:2048], in_=src[:, :, 1024:2048])
-            elif unit in OPT["halved"]:
+            if in_halves:
                 nc.sync.dma_start(out=dst[:, 0:1, :], in_=src[:, 0:1, :])
                 nc.sync.dma_start(out=dst[:, 1:2, :], in_=src[:, 1:2, :])
             else:
                 nc.sync.dma_start(out=dst, in_=src)
 
-        def next_load():
-            i = state["later"]
-            if i < len(later):
-                state["later"] = i + 1
-                load(later[i])
+        def load_next_chunk():
+            i = progress["loads"]
+            if 4 + i < len(ROUNDS):
+                progress["loads"] = i + 1
+                load_chunk(ROUNDS[4 + i], False)
 
-        def evac(eng, out, in_):
-            if eng == "s":
+        load_chunk(ROUNDS[0], True)
+        load_rows("x", x, loads.tile([P, LOAD_COLS], BF16, name="ld", tag="ld"), True)
+        load_rows("h", h_prev, loads.tile([P, LOAD_COLS], BF16, name="ld", tag="ld"), True)
+        load_chunk(ROUNDS[1], True)
+        load_chunk(ROUNDS[2], False)
+        load_chunk(ROUNDS[3], False)
+        load_rows("pp", potential_prev, pp_sb, False)
+
+        def copy_out(engine, out, in_):
+            if engine == "scalar":
                 nc.scalar.copy(out=out, in_=in_)
             else:
                 nc.vector.tensor_copy(out=out, in_=in_)
 
-        def four_transposes(words, first, alternate):
+        def transpose_two_passes(words, start_word, first_is_pass_0, grouped_words, engine):
             bank = tp_pool.tile([P, 4, P], F32, name="tpb", tag="tp")
             for j in range(4):
-                if alternate and j < 2:
-                    cols = words[:, first : first + 2 * P].rearrange("p (q u) -> p u q", u=2)[:, j, :]
+                if first_is_pass_0 and j < 2:
+                    cols = words[:, start_word : start_word + 2 * P].rearrange("p (q u) -> p u q", u=2)[:, j, :]
                 else:
-                    cols = words[:, first + P * j : first + P * (j + 1)]
+                    cols = words[:, start_word + P * j : start_word + P * (j + 1)]
                 nc.tensor.transpose(bank[:, j, :], cols, ident[:])
-            return bank
+            copy_out(engine, grouped_words, bank[:].rearrange("q (g u) c -> q g c u", u=2))
 
-        def vectors_in():
-            vbank = tp_pool.tile([P, 4, P], F32, name="vbank", tag="tp")
-            nc.tensor.transpose(vbank[:, 0, :], vt[:].bitcast(F32), ident[:])
-            nc.vector.tensor_copy(out=vw[:], in_=vbank[:, 0, 0:32])
-            nc.vector.tensor_copy(out=vf[:], in_=vw[:].bitcast(BF16))
-            nc.vector.tensor_scalar_mul(out=vh[:], in0=vf[:, 8:16], scalar1=0.5)
-
-        def vcol(v, ti):
-            return vf[:, 8 * v + ti : 8 * v + ti + 1]
-
-        def activations_in(key, bs, quantise):
-            if key == "x":
-                if "xg" not in held:
-                    held["xg"] = keep.tile([P, 2, NB, 4], BF16, name="xg", tag="xr", align_bytes=64)
-                grouped = held["xg"]
-                g0 = 0
-            else:
-                grouped = hg
-                g0 = 2
+        def transpose_rows(key, grouped, row_blocks):
             words = loaded[key][:].bitcast(F32)
-            gf = grouped[:].bitcast(F32)
-            for b in bs:
-                bank = four_transposes(words, 512 * b, g0 == 0)
-                evac(
-                    "s" if b % 2 == 0 else "v",
-                    gf[:, :, P * b : P * (b + 1), :],
-                    bank[:].rearrange("q (g u) c -> q g c u", u=2),
+            grouped_words = grouped[:].bitcast(F32)
+            for b in row_blocks:
+                transpose_two_passes(
+                    words,
+                    ROW_WORDS * b,
+                    key == "x",
+                    grouped_words[:, :, P * b : P * (b + 1), :],
+                    "scalar" if b % 2 == 0 else "vector",
                 )
-            if 3 in bs:
-                next_load()
-            if not quantise:
-                return
+
+        def quantise_rows(grouped, first_pass):
             for g in range(2):
                 nc.vector.quantize_mx(
-                    out=cw[:, g0 + g, :].bitcast(FP8X4),
-                    scales=cs[:, g0 + g, :],
+                    out=act_codes[:, first_pass + g, :].bitcast(FP8X4),
+                    scales=act_scales[:, first_pass + g, :],
                     in_=grouped[:, g].rearrange("p c t -> p (c t)"),
                 )
 
-        def transposes_w(unit, e, half, eng):
+        def transpose_tile(unit, e, engines):
             words = loaded[unit][:].bitcast(F32)
-            if (unit, e) not in held:
-                held[(unit, e)] = wq.tile([P, 4, P, 4], BF16, name="wg", tag="wg", align_bytes=64)
-            gf = held[(unit, e)][:].bitcast(F32)
-            bank = four_transposes(words, 1024 * e + 512 * half, half == 0)
-            evac(eng, gf[:, 2 * half : 2 * half + 2, :, :], bank[:].rearrange("q (g u) c -> q g c u", u=2))
+            grouped = wq.tile([P, PASSES, P, 4], BF16, name="wg", tag="wg", align_bytes=MX_ALIGN)
+            held[("grouped", unit, e)] = grouped
+            grouped_words = grouped[:].bitcast(F32)
+            for pair in range(2):
+                transpose_two_passes(
+                    words,
+                    PAIR_WORDS * (2 * e + pair),
+                    pair == 0,
+                    grouped_words[:, 2 * pair : 2 * pair + 2, :, :],
+                    engines[pair],
+                )
 
-        def quantise_w(unit, e, g_lo, g_hi):
-            if ("q", unit, e) not in held:
-                ww_new = wq.tile([P, 4, P], U32, name="ww", tag="ww", align_bytes=64)
-                ws_new = wq.tile([P, 4, P], U8, name="ws", tag="ws", align_bytes=64)
-                held[("q", unit, e)] = (ww_new, ws_new)
-            ww, ws = held[("q", unit, e)]
+        def quantise_tile(unit, e):
+            codes = wq.tile([P, PASSES, P], U32, name="ww", tag="ww", align_bytes=MX_ALIGN)
+            scales = wq.tile([P, PASSES, P], U8, name="ws", tag="ws", align_bytes=MX_ALIGN)
+            held[("codes", unit, e)] = (codes, scales)
             nc.vector.quantize_mx(
-                out=ww[:, g_lo:g_hi, :].rearrange("p g c -> p (g c)").bitcast(FP8X4),
-                scales=ws[:, g_lo:g_hi, :].rearrange("p g c -> p (g c)"),
-                in_=held[(unit, e)][:, g_lo:g_hi].rearrange("p g c t -> p (g c t)"),
+                out=codes[:].rearrange("p g c -> p (g c)").bitcast(FP8X4),
+                scales=scales[:].rearrange("p g c -> p (g c)"),
+                in_=held[("grouped", unit, e)][:].rearrange("p g c t -> p (g c t)"),
             )
 
-        def potential_in(a):
+        def vectors_to_partitions():
+            bank = tp_pool.tile([P, 4, P], F32, name="vbank", tag="tp")
+            nc.tensor.transpose(bank[:, 0, :], vec_rows[:].bitcast(F32), ident[:])
+            nc.vector.tensor_copy(out=vec_words[:], in_=bank[:, 0, 0:32])
+            nc.vector.tensor_copy(out=vec_f32[:], in_=vec_words[:].bitcast(BF16))
+            nc.vector.tensor_scalar_mul(out=half_b_z[:], in0=vec_f32[:, 8 * B_Z : 8 * B_Z + 8], scalar1=0.5)
+
+        def per_partition(v, ti):
+            return vec_f32[:, 8 * v + ti : 8 * v + ti + 1]
+
+        def potential_chunk(a):
             words = pp_sb[:].bitcast(F32)
             bank = bk_pool.tile([P, 4, P], F32, name="ppb", tag="bk")
             for b in range(4):
-                nc.tensor.transpose(bank[:, b, :], words[:, 512 * b + P * a : 512 * b + P * (a + 1)], ident[:])
+                start_word = ROW_WORDS * b + P * a
+                nc.tensor.transpose(bank[:, b, :], words[:, start_word : start_word + P], ident[:])
+            t0 = 2 * (a % 2)
             nc.vector.tensor_tensor(
-                out=sT[:, 2 * a : 2 * a + 2, :],
+                out=base[:, 2 * a : 2 * a + 2, :],
                 in0=bank[:].rearrange("q b c -> q (b c)").bitcast(BF16).rearrange("q (c e) -> q e c", e=2),
-                in1=hg[:, a // 2, :, 2 * (a % 2) : 2 * (a % 2) + 2].rearrange("q c e -> q e c"),
+                in1=h_grouped[:, a // 2, :, t0 : t0 + 2].rearrange("q c e -> q e c"),
                 op=ALU.add,
             )
 
-        def passes(unit, e, gs):
+        def multiply(unit, e, passes):
             gate, a = unit
             ti = 2 * a + e
-            ww, ws = held[("q", unit, e)]
-            if gs[0] == 0:
-                held[("acc", unit, e)] = acc_pool.tile([P, NB], F32, name="acc", tag="acc")
+            codes, scales = held[("codes", unit, e)]
+            if passes[0] == 0:
+                held[("acc", unit, e)] = acc_pool.tile([P, BATCH], F32, name="acc", tag="acc")
             acc = held[("acc", unit, e)]
-            for g in gs:
+            for g in passes:
                 if gate == "c" and g >= 2:
-                    rhs, rsc = rw[:, g - 2, :], rs[:, g - 2, :]
+                    rhs, rhs_scale = rh_codes[:, g - 2, :], rh_scales[:, g - 2, :]
                 else:
-                    rhs, rsc = cw[:, g, :], cs[:, g, :]
+                    rhs, rhs_scale = act_codes[:, g, :], act_scales[:, g, :]
                 nc.tensor.matmul_mx(
                     out=acc[:],
-                    lhsT=ww[:, g, :].bitcast(FP8X4),
-                    lhsT_scale=ws[:, g, :],
+                    lhsT=codes[:, g, :].bitcast(FP8X4),
+                    lhsT_scale=scales[:, g, :],
                     rhs=rhs.bitcast(FP8X4),
-                    rhs_scale=rsc,
+                    rhs_scale=rhs_scale,
                     start=(g == 0),
-                    stop=(g == 3),
+                    stop=(g == PASSES - 1),
                 )
-            if gs[-1] != 3:
+            if passes[-1] != PASSES - 1:
                 return
             if gate == "r":
-                nc.scalar.activation(out=r_all[:, ti, :], in_=acc[:], func=ACT.Sigmoid, bias=vcol(0, ti), scale=1.0)
+                nc.scalar.activation(
+                    out=r_all[:, ti, :], in_=acc[:], func=ACT.Sigmoid, bias=per_partition(B_R, ti), scale=1.0
+                )
             elif gate == "c":
-                d = work.tile([P, NB], F32, name="d", tag="d")
-                nc.scalar.activation(out=d[:], in_=acc[:], func=ACT.Tanh, bias=vcol(2, ti), scale=1.0)
-                held[("d", ti)] = d
+                blend = work.tile([P, BATCH], F32, name="d", tag="d")
+                nc.scalar.activation(out=blend[:], in_=acc[:], func=ACT.Tanh, bias=per_partition(B_C, ti), scale=1.0)
+                held[("blend", ti)] = blend
             else:
-                zt = work.tile([P, NB], F32, name="zt", tag="zt")
-                nc.scalar.activation(out=zt[:], in_=acc[:], func=ACT.Tanh, bias=vh[:, ti : ti + 1], scale=0.5)
-                held[("z", ti)] = zt
+                tanh_z = work.tile([P, BATCH], F32, name="zt", tag="zt")
+                nc.scalar.activation(out=tanh_z[:], in_=acc[:], func=ACT.Tanh, bias=half_b_z[:, ti : ti + 1], scale=0.5)
+                held[("tanh_z", ti)] = tanh_z
 
         def reset_times_hidden(g):
             if g == 0:
-                held["rhg"] = keep.tile([P, 2, NB, 4], BF16, name="rhg", tag="xr", align_bytes=64)
-            rhg = held["rhg"]
+                held["rh_grouped"] = keep.tile([P, 2, BATCH, 4], BF16, name="rhg", tag="xr", align_bytes=MX_ALIGN)
+            rh_grouped = held["rh_grouped"]
             nc.vector.tensor_tensor(
-                out=rhg[:, g],
+                out=rh_grouped[:, g],
                 in0=r_all[:, 4 * g : 4 * g + 4, :].rearrange("p t c -> p c t"),
-                in1=hg[:, g],
+                in1=h_grouped[:, g],
                 op=ALU.mult,
             )
             nc.vector.quantize_mx(
-                out=rw[:, g, :].bitcast(FP8X4),
-                scales=rs[:, g, :],
-                in_=rhg[:, g].rearrange("p c t -> p (c t)"),
+                out=rh_codes[:, g, :].bitcast(FP8X4),
+                scales=rh_scales[:, g, :],
+                in_=rh_grouped[:, g].rearrange("p c t -> p (c t)"),
             )
 
         def candidate_minus_hidden(a):
             for ti in (2 * a, 2 * a + 1):
-                d = held[("d", ti)]
-                nc.vector.tensor_tensor(out=d[:], in0=d[:], in1=hg[:, ti // 4, :, ti % 4], op=ALU.subtract)
-
-        def new_tiles(a):
-            for ti in (2 * a, 2 * a + 1):
-                held[("pot", ti)] = work.tile([P, NB], F32, name="pot", tag="pot")
-                for kind in ("av", "ng"):
-                    held[(kind, ti)] = late.tile([P, NB], F32, name=kind, tag=kind)
-
-        def part1(a, cols, scalar_decay):
-            tis = (2 * a, 2 * a + 1)
-            for ti in tis:
-                d = held[("d", ti)]
-                nc.vector.scalar_tensor_tensor(
-                    out=d[:, cols], in0=held[("z", ti)][:, cols], scalar=1.0, in1=d[:, cols], op0=ALU.add, op1=ALU.mult
+                blend = held[("blend", ti)]
+                nc.vector.tensor_tensor(
+                    out=blend[:], in0=blend[:], in1=h_grouped[:, ti // 4, :, ti % 4], op=ALU.subtract
                 )
-            for ti in tis:
+
+        def result_tiles(a):
+            for ti in (2 * a, 2 * a + 1):
+                for kind in ("pot", "av", "ng"):
+                    held[(kind, ti)] = work.tile([P, BATCH], F32, name=kind, tag=kind)
+
+        def potential_and_activated(a, cols):
+            tiles = (2 * a, 2 * a + 1)
+            for ti in tiles:
+                blend = held[("blend", ti)]
                 nc.vector.scalar_tensor_tensor(
-                    out=held[("pot", ti)][:, cols], in0=held[("d", ti)][:, cols], scalar=0.5, in1=sT[:, ti, cols],
+                    out=blend[:, cols], in0=held[("tanh_z", ti)][:, cols], scalar=1.0, in1=blend[:, cols],
+                    op0=ALU.add, op1=ALU.mult,
+                )
+            for ti in tiles:
+                nc.vector.scalar_tensor_tensor(
+                    out=held[("pot", ti)][:, cols], in0=held[("blend", ti)][:, cols], scalar=0.5, in1=base[:, ti, cols],
                     op0=ALU.mult, op1=ALU.add,
                 )
-            if scalar_decay:
-                for ti in tis:
+            if a in DECAY_ON_SCALAR:
+                for ti in tiles:
                     nc.scalar.activation(
-                        out=held[("ng", ti)][:, cols], in_=held[("pot", ti)][:, cols], func=ACT.Copy, scale=vcol(4, ti)
+                        out=held[("ng", ti)][:, cols], in_=held[("pot", ti)][:, cols], func=ACT.Copy,
+                        scale=per_partition(DECAY, ti),
                     )
-            for ti in tis:
+            for ti in tiles:
                 pot = held[("pot", ti)]
                 nc.vector.scalar_tensor_tensor(
-                    out=held[("av", ti)][:, cols], in0=pot[:, cols], scalar=vcol(3, ti), in1=pot[:, cols],
+                    out=held[("av", ti)][:, cols], in0=pot[:, cols], scalar=per_partition(TRESH, ti), in1=pot[:, cols],
                     op0=ALU.is_gt, op1=ALU.mult,
                 )
 
-        def part2(a, cols, scalar_decay):
-            tis = (2 * a, 2 * a + 1)
-            if scalar_decay:
-                for ti in tis:
+        def non_gated(a, cols):
+            tiles = (2 * a, 2 * a + 1)
+            if a in DECAY_ON_SCALAR:
+                for ti in tiles:
                     ng = held[("ng", ti)]
                     nc.vector.scalar_tensor_tensor(
-                        out=ng[:, cols], in0=held[("pot", ti)][:, cols], scalar=vcol(3, ti), in1=ng[:, cols],
-                        op0=ALU.is_le, op1=ALU.mult,
+                        out=ng[:, cols], in0=held[("pot", ti)][:, cols], scalar=per_partition(TRESH, ti),
+                        in1=ng[:, cols], op0=ALU.is_le, op1=ALU.mult,
                     )
                 return
-            for ti in tis:
+            for ti in tiles:
                 nc.vector.tensor_scalar(
-                    out=held[("ng", ti)][:, cols], in0=held[("pot", ti)][:, cols], scalar1=vcol(3, ti),
-                    scalar2=vcol(4, ti), op0=ALU.is_le, op1=ALU.mult,
+                    out=held[("ng", ti)][:, cols], in0=held[("pot", ti)][:, cols], scalar1=per_partition(TRESH, ti),
+                    scalar2=per_partition(DECAY, ti), op0=ALU.is_le, op1=ALU.mult,
                 )
-            for ti in tis:
+            for ti in tiles:
                 ng = held[("ng", ti)]
                 nc.vector.tensor_tensor(out=ng[:, cols], in0=ng[:, cols], in1=held[("pot", ti)][:, cols], op=ALU.mult)
 
         dram_of = {"av": out_0, "ng": out_1}
 
-        def back_half(kind, a, hb, eng, store):
-            if hb == 0:
-                held[("o", kind)] = outs.tile([P, 4, 256], F32, name="o" + kind, tag="o" + kind)
-            o = held[("o", kind)]
+        def back_to_rows(kind, a, half, engine, store_each_half):
+            if half == 0:
+                held[("rows", kind)] = outs.tile([P, 4, CHUNK], F32, name="o" + kind, tag="o" + kind)
+            rows = held[("rows", kind)]
             bank = bk_pool.tile([P, 2, 2, P], F32, name="bkb", tag="bk")
             for b2 in range(2):
                 for e in range(2):
-                    b = 2 * hb + b2
+                    b = 2 * half + b2
                     nc.tensor.transpose(bank[:, b2, e, :], held[(kind, 2 * a + e)][:, P * b : P * (b + 1)], ident[:])
-            evac(
-                eng,
-                o[:, 2 * hb : 2 * hb + 2, :].rearrange("c b (q e) -> c b q e", e=2),
+            copy_out(
+                engine,
+                rows[:, 2 * half : 2 * half + 2, :].rearrange("c b (q e) -> c b q e", e=2),
                 bank[:].rearrange("c b e q -> c b q e"),
             )
             view = dram_of[kind].rearrange("(c b) h -> c b h", b=4)
-            if store == "half":
+            if store_each_half:
                 nc.sync.dma_start(
-                    out=view[:, 2 * hb : 2 * hb + 2, 256 * a : 256 * (a + 1)], in_=o[:, 2 * hb : 2 * hb + 2, :]
+                    out=view[:, 2 * half : 2 * half + 2, CHUNK * a : CHUNK * (a + 1)],
+                    in_=rows[:, 2 * half : 2 * half + 2, :],
                 )
-            elif hb == 1:
-                nc.sync.dma_start(out=view[:, :, 256 * a : 256 * (a + 1)], in_=o[:])
+            elif half == 1:
+                nc.sync.dma_start(out=view[:, :, CHUNK * a : CHUNK * (a + 1)], in_=rows[:])
 
-        zeros = consts.tile([P, NB], BF16, name="zeros")
-        nc.vector.memset(zeros[:], 0.0)
+        def back_whole(kind, a):
+            for half in range(2):
+                back_to_rows(kind, a, half, "scalar", False)
 
-        def keep_clock(n):
-            idle = acc_pool.tile([P, NB], F32, name="idle", tag="acc")
-            for i in range(n):
-                nc.tensor.matmul(out=idle[:], lhsT=zeros[:, 0:P], rhs=zeros[:], start=True, stop=True)
+        first, second = ROUNDS[0], ROUNDS[1]
+        for e in range(2):
+            transpose_tile(first, e, ("scalar", "vector"))
+            quantise_tile(first, e)
+        load_next_chunk()
+        x_grouped = keep.tile([P, 2, BATCH, 4], BF16, name="xg", tag="xr", align_bytes=MX_ALIGN)
+        transpose_rows("x", x_grouped, (0, 1, 2, 3))
+        load_next_chunk()
+        quantise_rows(x_grouped, 0)
+        transpose_rows("h", h_grouped, (0, 1))
+        for g in (0, 1):
+            for e in range(2):
+                multiply(first, e, (g,))
+        transpose_rows("h", h_grouped, (2, 3))
+        load_next_chunk()
+        quantise_rows(h_grouped, 2)
+        for e in range(2):
+            transpose_tile(second, e, ("scalar", "scalar"))
+        load_next_chunk()
+        vectors_to_partitions()
+        for e in range(2):
+            quantise_tile(second, e)
+        for g in (2, 3):
+            for e in range(2):
+                multiply(first, e, (g,))
 
-        whole = slice(0, NB)
-        for step in build_steps():
-            kind = step[0]
-            if kind == "WARM":
-                keep_clock(step[1])
-            elif kind == "LOADS":
-                for item in step[1]:
-                    load(item)
-            elif kind == "A":
-                activations_in(step[1], (0, 1, 2, 3), True)
-            elif kind == "Ah":
-                activations_in(step[1], (2 * step[2], 2 * step[2] + 1), False)
-            elif kind == "Aq":
-                activations_in(step[1], (), True)
-            elif kind == "VEC":
-                vectors_in()
-            elif kind == "T":
-                transposes_w(step[1], step[2], step[3], step[4])
-            elif kind == "FREE":
-                next_load()
-            elif kind == "Q":
-                quantise_w(step[1], step[2], 0, 4)
-            elif kind == "Qh":
-                quantise_w(step[1], step[2], 2 * step[3], 2 * step[3] + 2)
-            elif kind == "M":
-                passes(step[1], step[2], step[3])
-            elif kind == "PP":
-                potential_in(step[1])
-            elif kind == "RH":
-                reset_times_hidden(step[1])
-            elif kind == "D":
-                candidate_minus_hidden(step[1])
-            elif kind == "P1":
-                new_tiles(step[1])
-                part1(step[1], whole, step[1] in OPT["scalar_decay"])
-            elif kind == "P2":
-                part2(step[1], whole, step[1] in OPT["scalar_decay"])
-            elif kind == "B":
-                for hb in range(2):
-                    back_half(step[1], step[2], hb, "s", "whole")
-            elif kind == "LAST":
-                new_tiles(3)
-                for hb in range(2):
-                    cols = slice(256 * hb, 256 * (hb + 1))
-                    part1(3, cols, True)
-                    part2(3, cols, True)
-                    for a in OPT.get("defer", ()):
-                        for hb2 in range(2):
-                            back_half(("av", "ng")[hb], a, hb2, "s", "whole")
-                    back_half("av", 3, hb, "s", "half")
-                    back_half("ng", 3, hb, "s" if hb == 0 else "v", "half")
+        whole = slice(0, BATCH)
+        all_passes = (0, 1, 2, 3)
+        complete = {}
+        for a in range(LAST_CHUNK):
+            complete[max(ROUNDS.index(("c", a)), ROUNDS.index(("z", a)))] = a
+        for i in range(1, len(ROUNDS)):
+            if i in POTENTIAL_BEFORE:
+                potential_chunk(POTENTIAL_BEFORE[i])
+            if i + 1 < len(ROUNDS):
+                for e in range(2):
+                    transpose_tile(ROUNDS[i + 1], e, ("scalar", "scalar"))
+                load_next_chunk()
+            if i - 2 in complete:
+                back_whole("av", complete[i - 2])
+            if i - 3 in complete:
+                back_whole("ng", complete[i - 3])
+            if i - 1 in complete:
+                result_tiles(complete[i - 1])
+                potential_and_activated(complete[i - 1], whole)
+            if i - 2 in complete:
+                non_gated(complete[i - 2], whole)
+            if i + 1 < len(ROUNDS):
+                for e in range(2):
+                    quantise_tile(ROUNDS[i + 1], e)
+            for e in range(2):
+                multiply(ROUNDS[i], e, all_passes)
+            gate, a = ROUNDS[i]
+            if gate == "r" and a % 2 == 1:
+                reset_times_hidden(a // 2)
+            if gate == "c":
+                candidate_minus_hidden(a)
+
+        back_whole("ng", complete[len(ROUNDS) - 3])
+        result_tiles(LAST_CHUNK)
+        for half in range(2):
+            cols = slice(HALF * half, HALF * (half + 1))
+            potential_and_activated(LAST_CHUNK, cols)
+            non_gated(LAST_CHUNK, cols)
+            back_to_rows("av", LAST_CHUNK, half, "scalar", True)
+            back_to_rows("ng", LAST_CHUNK, half, "scalar" if half == 0 else "vector", True)

@@ -28,8 +28,8 @@ ROUNDS = [
     ("z", 0), ("c", 0), ("c", 1), ("z", 1), ("c", 2), ("z", 2), ("c", 3), ("z", 3),
 ]
 LAST_CHUNK = 3
-POTENTIAL_BEFORE = {2: 0, 3: 1, 4: 2, 5: 3}
-DECAY_ON_SCALAR = (2, 3)
+FIRST_POTENTIAL_ROUND = 2
+DECAY_ON_SCALAR_FROM = 2
 B_R = 0
 B_Z = 1
 B_C = 2
@@ -55,13 +55,13 @@ def tile_pglu_b_kernel(
 
         vec_rows = consts.tile([P, CHUNK], BF16, name="vec_rows")
         nc.vector.memset(vec_rows[:], 0.0)
+        for v, vec in enumerate((b_r, b_z, b_c, tresh, decay_rate)):
+            nc.scalar.dma_start(out=vec_rows[4 * v : 4 * v + 4, :], in_=vec.rearrange("(a q) -> a q", a=4))
         warm = consts.tile([P, 1], F32, name="warm")
         nc.vector.memset(warm[:], 0.0)
         nc.scalar.activation(out=warm[:], in_=warm[:], func=ACT.Sigmoid)
         ident = consts.tile([P, P], F32, name="ident")
         make_identity(nc, ident[:])
-        for v, vec in enumerate((b_r, b_z, b_c, tresh, decay_rate)):
-            nc.gpsimd.dma_start(out=vec_rows[4 * v : 4 * v + 4, :], in_=vec.rearrange("(a q) -> a q", a=4))
         vec_words = consts.tile([P, 32], F32, name="vec_words")
         vec_f32 = consts.tile([P, 64], F32, name="vec_f32")
         half_b_z = consts.tile([P, 8], F32, name="half_b_z")
@@ -275,7 +275,7 @@ def tile_pglu_b_kernel(
                     out=held[("pot", ti)][:, cols], in0=held[("blend", ti)][:, cols], scalar=0.5, in1=base[:, ti, cols],
                     op0=ALU.mult, op1=ALU.add,
                 )
-            if a in DECAY_ON_SCALAR:
+            if a >= DECAY_ON_SCALAR_FROM:
                 for ti in tiles:
                     nc.scalar.activation(
                         out=held[("ng", ti)][:, cols], in_=held[("pot", ti)][:, cols], func=ACT.Copy,
@@ -290,7 +290,7 @@ def tile_pglu_b_kernel(
 
         def non_gated(a, cols):
             tiles = (2 * a, 2 * a + 1)
-            if a in DECAY_ON_SCALAR:
+            if a >= DECAY_ON_SCALAR_FROM:
                 for ti in tiles:
                     ng = held[("ng", ti)]
                     nc.vector.scalar_tensor_tensor(
@@ -368,8 +368,8 @@ def tile_pglu_b_kernel(
         for a in range(LAST_CHUNK):
             complete[max(ROUNDS.index(("c", a)), ROUNDS.index(("z", a)))] = a
         for i in range(1, len(ROUNDS)):
-            if i in POTENTIAL_BEFORE:
-                potential_chunk(POTENTIAL_BEFORE[i])
+            if 0 <= i - FIRST_POTENTIAL_ROUND < 4:
+                potential_chunk(i - FIRST_POTENTIAL_ROUND)
             if i + 1 < len(ROUNDS):
                 for e in range(2):
                     transpose_tile(ROUNDS[i + 1], e, ("scalar", "scalar"))

from contextlib import ExitStack

import concourse.mybir as mybir
from concourse.masks import make_identity

FLOPS = 3 * 2 * 512 * 1024 * 2048

F32 = mybir.dt.float32
BF16 = mybir.dt.bfloat16
U32 = mybir.dt.uint32
U8 = mybir.dt.uint8
FP8X4 = mybir.dt.float8_e4m3fn_x4
ACT = mybir.ActivationFunctionType
ALU = mybir.AluOpType

P = 128
BATCH = 512
HALF = BATCH // 2
CHUNK = 256
PASSES = 4
LOAD_COLS = 4096
ROW_WORDS = 512
PAIR_WORDS = 512
MX_ALIGN = 64
LOAD_SLOTS = 8
ROUNDS = [
    ("r", 0), ("r", 1), ("r", 2), ("r", 3),
    ("z", 0), ("c", 0), ("c", 1), ("z", 1), ("c", 2), ("z", 2), ("c", 3), ("z", 3),
]
LAST_CHUNK = 3
FIRST_POTENTIAL_ROUND = 2
DECAY_ON_SCALAR_FROM = 2
B_R = 0
B_Z = 1
B_C = 2
TRESH = 3
DECAY = 4


def tile_pglu_b_kernel(
    tc, x, h_prev, potential_prev, W_r, b_r, W_z, b_z, W_c, b_c, tresh, decay_rate, out_0, out_1
):
    nc = tc.nc
    with ExitStack() as ctx:
        ctx.enter_context(tc.manual_schedule())
        consts = ctx.enter_context(tc.tile_pool(name="consts", bufs=1))
        keep = ctx.enter_context(tc.tile_pool(name="keep", bufs=1))
        loads = ctx.enter_context(tc.tile_pool(name="loads", bufs=LOAD_SLOTS))
        wq = ctx.enter_context(tc.tile_pool(name="wq", bufs=4))
        work = ctx.enter_context(tc.tile_pool(name="work", bufs=4))
        outs = ctx.enter_context(tc.tile_pool(name="outs", bufs=2))
        tp_pool = ctx.enter_context(tc.psum_pool(name="tp", bufs=4))
        bk_pool = ctx.enter_context(tc.psum_pool(name="bk", bufs=2))
        acc_pool = ctx.enter_context(tc.psum_pool(name="acc", bufs=2))

        vec_rows = consts.tile([P, CHUNK], BF16, name="vec_rows")
        nc.vector.memset(vec_rows[:], 0.0)
        for v, vec in enumerate((b_r, b_z, b_c, tresh, decay_rate)):
            nc.scalar.dma_start(out=vec_rows[4 * v : 4 * v + 4, :], in_=vec.rearrange("(a q) -> a q", a=4))
        warm = consts.tile([P, 1], F32, name="warm")
        nc.vector.memset(warm[:], 0.0)
        nc.scalar.activation(out=warm[:], in_=warm[:], func=ACT.Sigmoid)
        ident = consts.tile([P, P], F32, name="ident")
        make_identity(nc, ident[:])
        vec_words = consts.tile([P, 32], F32, name="vec_words")
        vec_f32 = consts.tile([P, 64], F32, name="vec_f32")
        half_b_z = consts.tile([P, 8], F32, name="half_b_z")

        h_grouped = keep.tile([P, 2, BATCH, 4], BF16, name="h_grouped", align_bytes=MX_ALIGN)
        act_codes = keep.tile([P, PASSES, BATCH], U32, name="act_codes", align_bytes=MX_ALIGN)
        act_scales = keep.tile([P, PASSES, BATCH], U8, name="act_scales", align_bytes=MX_ALIGN)
        rh_codes = keep.tile([P, 2, BATCH], U32, name="rh_codes", align_bytes=MX_ALIGN)
        rh_scales = keep.tile([P, 2, BATCH], U8, name="rh_scales", align_bytes=MX_ALIGN)
        r_all = keep.tile([P, 8, BATCH], F32, name="r_all")
        base = keep.tile([P, 8, BATCH], F32, name="base")
        pp_sb = keep.tile([P, LOAD_COLS], BF16, name="pp_sb")

        weight_of = {"r": W_r, "z": W_z, "c": W_c}
        loaded = {}
        held = {}
        progress = {"loads": 0}

        def load_rows(key, source, tile_ap, in_halves):
            loaded[key] = tile_ap
            src = source.rearrange("(p b) k -> p b k", b=4)
            dst = tile_ap[:].rearrange("p (b k) -> p b k", b=4)
            if in_halves:
                nc.sync.dma_start(out=dst[:, 0:2, :], in_=src[:, 0:2, :])
                nc.sync.dma_start(out=dst[:, 2:4, :], in_=src[:, 2:4, :])
            else:
                nc.sync.dma_start(out=dst, in_=src)

        def load_chunk(unit, in_halves):
            loaded[unit] = loads.tile([P, LOAD_COLS], BF16, name="ld", tag="ld")
            src = weight_of[unit[0]].rearrange("(a p e) k -> a p e k", a=4, e=2)[unit[1]]
            dst = loaded[unit][:].rearrange("p (e k) -> p e k", e=2)
            if in_halves:
                nc.sync.dma_start(out=dst[:, 0:1, :], in_=src[:, 0:1, :])
                nc.sync.dma_start(out=dst[:, 1:2, :], in_=src[:, 1:2, :])
            else:
                nc.sync.dma_start(out=dst, in_=src)

        def load_next_chunk():
            i = progress["loads"]
            if 4 + i < len(ROUNDS):
                progress["loads"] = i + 1
                load_chunk(ROUNDS[4 + i], False)

        load_chunk(ROUNDS[0], True)
        load_rows("x", x, loads.tile([P, LOAD_COLS], BF16, name="ld", tag="ld"), True)
        load_rows("h", h_prev, loads.tile([P, LOAD_COLS], BF16, name="ld", tag="ld"), True)
        load_chunk(ROUNDS[1], True)
        load_chunk(ROUNDS[2], False)
        load_chunk(ROUNDS[3], False)
        load_rows("pp", potential_prev, pp_sb, False)

        def copy_out(engine, out, in_):
            if engine == "scalar":
                nc.scalar.copy(out=out, in_=in_)
            else:
                nc.vector.tensor_copy(out=out, in_=in_)

        def transpose_two_passes(words, start_word, first_is_pass_0, grouped_words, engine):
            bank = tp_pool.tile([P, 4, P], F32, name="tpb", tag="tp")
            for j in range(4):
                if first_is_pass_0 and j < 2:
                    cols = words[:, start_word : start_word + 2 * P].rearrange("p (q u) -> p u q", u=2)[:, j, :]
                else:
                    cols = words[:, start_word + P * j : start_word + P * (j + 1)]
                nc.tensor.transpose(bank[:, j, :], cols, ident[:])
            copy_out(engine, grouped_words, bank[:].rearrange("q (g u) c -> q g c u", u=2))

        def transpose_rows(key, grouped, row_blocks):
            words = loaded[key][:].bitcast(F32)
            grouped_words = grouped[:].bitcast(F32)
            for b in row_blocks:
                transpose_two_passes(
                    words,
                    ROW_WORDS * b,
                    key == "x",
                    grouped_words[:, :, P * b : P * (b + 1), :],
                    "scalar" if b % 2 == 0 else "vector",
                )

        def quantise_rows(grouped, first_pass):
            for g in range(2):
                nc.vector.quantize_mx(
                    out=act_codes[:, first_pass + g, :].bitcast(FP8X4),
                    scales=act_scales[:, first_pass + g, :],
                    in_=grouped[:, g].rearrange("p c t -> p (c t)"),
                )

        def transpose_tile(unit, e, engines):
            words = loaded[unit][:].bitcast(F32)
            grouped = wq.tile([P, PASSES, P, 4], BF16, name="wg", tag="wg", align_bytes=MX_ALIGN)
            held[("grouped", unit, e)] = grouped
            grouped_words = grouped[:].bitcast(F32)
            for pair in range(2):
                transpose_two_passes(
                    words,
                    PAIR_WORDS * (2 * e + pair),
                    pair == 0,
                    grouped_words[:, 2 * pair : 2 * pair + 2, :, :],
                    engines[pair],
                )

        def quantise_tile(unit, e):
            codes = wq.tile([P, PASSES, P], U32, name="ww", tag="ww", align_bytes=MX_ALIGN)
            scales = wq.tile([P, PASSES, P], U8, name="ws", tag="ws", align_bytes=MX_ALIGN)
            held[("codes", unit, e)] = (codes, scales)
            nc.vector.quantize_mx(
                out=codes[:].rearrange("p g c -> p (g c)").bitcast(FP8X4),
                scales=scales[:].rearrange("p g c -> p (g c)"),
                in_=held[("grouped", unit, e)][:].rearrange("p g c t -> p (g c t)"),
            )

        def vectors_to_partitions():
            bank = tp_pool.tile([P, 4, P], F32, name="vbank", tag="tp")
            nc.tensor.transpose(bank[:, 0, :], vec_rows[:].bitcast(F32), ident[:])
            nc.vector.tensor_copy(out=vec_words[:], in_=bank[:, 0, 0:32])
            nc.vector.tensor_copy(out=vec_f32[:], in_=vec_words[:].bitcast(BF16))
            nc.vector.tensor_scalar_mul(out=half_b_z[:], in0=vec_f32[:, 8 * B_Z : 8 * B_Z + 8], scalar1=0.5)

        def per_partition(v, ti):
            return vec_f32[:, 8 * v + ti : 8 * v + ti + 1]

        def potential_chunk(a):
            words = pp_sb[:].bitcast(F32)
            bank = bk_pool.tile([P, 4, P], F32, name="ppb", tag="bk")
            for b in range(4):
                start_word = ROW_WORDS * b + P * a
                nc.tensor.transpose(bank[:, b, :], words[:, start_word : start_word + P], ident[:])
            t0 = 2 * (a % 2)
            nc.vector.tensor_tensor(
                out=base[:, 2 * a : 2 * a + 2, :],
                in0=bank[:].rearrange("q b c -> q (b c)").bitcast(BF16).rearrange("q (c e) -> q e c", e=2),
                in1=h_grouped[:, a // 2, :, t0 : t0 + 2].rearrange("q c e -> q e c"),
                op=ALU.add,
            )

        def multiply(unit, e, passes):
            gate, a = unit
            ti = 2 * a + e
            codes, scales = held[("codes", unit, e)]
            if passes[0] == 0:
                held[("acc", unit, e)] = acc_pool.tile([P, BATCH], F32, name="acc", tag="acc")
            acc = held[("acc", unit, e)]
            for g in passes:
                if gate == "c" and g >= 2:
                    rhs, rhs_scale = rh_codes[:, g - 2, :], rh_scales[:, g - 2, :]
                else:
                    rhs, rhs_scale = act_codes[:, g, :], act_scales[:, g, :]
                nc.tensor.matmul_mx(
                    out=acc[:],
                    lhsT=codes[:, g, :].bitcast(FP8X4),
                    lhsT_scale=scales[:, g, :],
                    rhs=rhs.bitcast(FP8X4),
                    rhs_scale=rhs_scale,
                    start=(g == 0),
                    stop=(g == PASSES - 1),
                )
            if passes[-1] != PASSES - 1:
                return
            if gate == "r":
                nc.scalar.activation(
                    out=r_all[:, ti, :], in_=acc[:], func=ACT.Sigmoid, bias=per_partition(B_R, ti), scale=1.0
                )
            elif gate == "c":
                blend = work.tile([P, BATCH], F32, name="d", tag="d")
                nc.scalar.activation(out=blend[:], in_=acc[:], func=ACT.Tanh, bias=per_partition(B_C, ti), scale=1.0)
                held[("blend", ti)] = blend
            else:
                tanh_z = work.tile([P, BATCH], F32, name="zt", tag="zt")
                nc.scalar.activation(out=tanh_z[:], in_=acc[:], func=ACT.Tanh, bias=half_b_z[:, ti : ti + 1], scale=0.5)
                held[("tanh_z", ti)] = tanh_z

        def reset_times_hidden(g):
            if g == 0:
                held["rh_grouped"] = keep.tile([P, 2, BATCH, 4], BF16, name="rhg", tag="xr", align_bytes=MX_ALIGN)
            rh_grouped = held["rh_grouped"]
            nc.vector.tensor_tensor(
                out=rh_grouped[:, g],
                in0=r_all[:, 4 * g : 4 * g + 4, :].rearrange("p t c -> p c t"),
                in1=h_grouped[:, g],
                op=ALU.mult,
            )
            nc.vector.quantize_mx(
                out=rh_codes[:, g, :].bitcast(FP8X4),
                scales=rh_scales[:, g, :],
                in_=rh_grouped[:, g].rearrange("p c t -> p (c t)"),
            )

        def candidate_minus_hidden(a):
            for ti in (2 * a, 2 * a + 1):
                blend = held[("blend", ti)]
                nc.vector.tensor_tensor(
                    out=blend[:], in0=blend[:], in1=h_grouped[:, ti // 4, :, ti % 4], op=ALU.subtract
                )

        def result_tiles(a):
            for ti in (2 * a, 2 * a + 1):
                for kind in ("pot", "av", "ng"):
                    held[(kind, ti)] = work.tile([P, BATCH], F32, name=kind, tag=kind)

        def potential_and_activated(a, cols):
            tiles = (2 * a, 2 * a + 1)
            for ti in tiles:
                blend = held[("blend", ti)]
                nc.vector.scalar_tensor_tensor(
                    out=blend[:, cols], in0=held[("tanh_z", ti)][:, cols], scalar=1.0, in1=blend[:, cols],
                    op0=ALU.add, op1=ALU.mult,
                )
            for ti in tiles:
                nc.vector.scalar_tensor_tensor(
                    out=held[("pot", ti)][:, cols], in0=held[("blend", ti)][:, cols], scalar=0.5, in1=base[:, ti, cols],
                    op0=ALU.mult, op1=ALU.add,
                )
            if a >= DECAY_ON_SCALAR_FROM:
                for ti in tiles:
                    nc.scalar.activation(
                        out=held[("ng", ti)][:, cols], in_=held[("pot", ti)][:, cols], func=ACT.Copy,
                        scale=per_partition(DECAY, ti),
                    )
            for ti in tiles:
                pot = held[("pot", ti)]
                nc.vector.scalar_tensor_tensor(
                    out=held[("av", ti)][:, cols], in0=pot[:, cols], scalar=per_partition(TRESH, ti), in1=pot[:, cols],
                    op0=ALU.is_gt, op1=ALU.mult,
                )

        def non_gated(a, cols):
            tiles = (2 * a, 2 * a + 1)
            if a >= DECAY_ON_SCALAR_FROM:
                for ti in tiles:
                    ng = held[("ng", ti)]
                    nc.vector.scalar_tensor_tensor(
                        out=ng[:, cols], in0=held[("pot", ti)][:, cols], scalar=per_partition(TRESH, ti),
                        in1=ng[:, cols], op0=ALU.is_le, op1=ALU.mult,
                    )
                return
            for ti in tiles:
                nc.vector.tensor_scalar(
                    out=held[("ng", ti)][:, cols], in0=held[("pot", ti)][:, cols], scalar1=per_partition(TRESH, ti),
                    scalar2=per_partition(DECAY, ti), op0=ALU.is_le, op1=ALU.mult,
                )
            for ti in tiles:
                ng = held[("ng", ti)]
                nc.vector.tensor_tensor(out=ng[:, cols], in0=ng[:, cols], in1=held[("pot", ti)][:, cols], op=ALU.mult)

        dram_of = {"av": out_0, "ng": out_1}

        def back_to_rows(kind, a, half, engine, store_each_half):
            if half == 0:
                held[("rows", kind)] = outs.tile([P, 4, CHUNK], F32, name="o" + kind, tag="o" + kind)
            rows = held[("rows", kind)]
            bank = bk_pool.tile([P, 2, 2, P], F32, name="bkb", tag="bk")
            for b2 in range(2):
                for e in range(2):
                    b = 2 * half + b2
                    nc.tensor.transpose(bank[:, b2, e, :], held[(kind, 2 * a + e)][:, P * b : P * (b + 1)], ident[:])
            copy_out(
                engine,
                rows[:, 2 * half : 2 * half + 2, :].rearrange("c b (q e) -> c b q e", e=2),
                bank[:].rearrange("c b e q -> c b q e"),
            )
            view = dram_of[kind].rearrange("(c b) h -> c b h", b=4)
            if store_each_half:
                nc.sync.dma_start(
                    out=view[:, 2 * half : 2 * half + 2, CHUNK * a : CHUNK * (a + 1)],
                    in_=rows[:, 2 * half : 2 * half + 2, :],
                )
            elif half == 1:
                nc.sync.dma_start(out=view[:, :, CHUNK * a : CHUNK * (a + 1)], in_=rows[:])

        def back_whole(kind, a):
            for half in range(2):
                back_to_rows(kind, a, half, "scalar", False)

        first, second = ROUNDS[0], ROUNDS[1]
        for e in range(2):
            transpose_tile(first, e, ("scalar", "vector"))
            quantise_tile(first, e)
        load_next_chunk()
        x_grouped = keep.tile([P, 2, BATCH, 4], BF16, name="xg", tag="xr", align_bytes=MX_ALIGN)
        transpose_rows("x", x_grouped, (0, 1, 2, 3))
        load_next_chunk()
        quantise_rows(x_grouped, 0)
        transpose_rows("h", h_grouped, (0, 1))
        for g in (0, 1):
            for e in range(2):
                multiply(first, e, (g,))
        transpose_rows("h", h_grouped, (2, 3))
        load_next_chunk()
        quantise_rows(h_grouped, 2)
        for e in range(2):
            transpose_tile(second, e, ("scalar", "scalar"))
        load_next_chunk()
        vectors_to_partitions()
        for e in range(2):
            quantise_tile(second, e)
        for g in (2, 3):
            for e in range(2):
                multiply(first, e, (g,))

        whole = slice(0, BATCH)
        all_passes = (0, 1, 2, 3)
        complete = {}
        for a in range(LAST_CHUNK):
            complete[max(ROUNDS.index(("c", a)), ROUNDS.index(("z", a)))] = a
        for i in range(1, len(ROUNDS)):
            if 0 <= i - FIRST_POTENTIAL_ROUND < 4:
                potential_chunk(i - FIRST_POTENTIAL_ROUND)
            if i + 1 < len(ROUNDS):
                for e in range(2):
                    transpose_tile(ROUNDS[i + 1], e, ("scalar", "scalar"))
                load_next_chunk()
            if i - 2 in complete:
                back_whole("av", complete[i - 2])
            if i - 3 in complete:
                back_whole("ng", complete[i - 3])
            if i - 1 in complete:
                result_tiles(complete[i - 1])
                potential_and_activated(complete[i - 1], whole)
            if i - 2 in complete:
                non_gated(complete[i - 2], whole)
            if i + 1 < len(ROUNDS):
                for e in range(2):
                    quantise_tile(ROUNDS[i + 1], e)
            for e in range(2):
                multiply(ROUNDS[i], e, all_passes)
            gate, a = ROUNDS[i]
            if gate == "r" and a % 2 == 1:
                reset_times_hidden(a // 2)
            if gate == "c":
                candidate_minus_hidden(a)

        back_whole("ng", complete[len(ROUNDS) - 3])
        result_tiles(LAST_CHUNK)
        for half in range(2):
            cols = slice(HALF * half, HALF * (half + 1))
            potential_and_activated(LAST_CHUNK, cols)
            non_gated(LAST_CHUNK, cols)
            back_to_rows("av", LAST_CHUNK, half, "scalar", True)
            back_to_rows("ng", LAST_CHUNK, half, "scalar" if half == 0 else "vector", True)
